import numpy as np
import ml_dtypes


def mxq(x, axis, fmt="e4m3"):
    dtype, down = {"e4m3": (ml_dtypes.float8_e4m3fn, 7), "e5m2": (ml_dtypes.float8_e5m2, 14)}[fmt]
    v = np.moveaxis(np.asarray(x, np.float32).astype(ml_dtypes.bfloat16).astype(np.float64), axis, -1)
    blocks = v.reshape(v.shape[:-1] + (-1, 32))
    amax = np.abs(blocks).max(-1, keepdims=True)
    byte = np.maximum(np.where(amax > 0, np.frexp(amax)[1] - 1 + 127, 0) - down, 1)
    scale = np.exp2(byte - 127.0)
    codes = (blocks / scale).astype(np.float32).astype(dtype).astype(np.float64)
    return np.moveaxis((codes * scale).reshape(v.shape), -1, axis)


WIDE = False


def mx_kscale(k):
    if not WIDE:
        return np.ones(k)
    levels = np.array([10, -10, 5, -5, 0])
    a = np.random.permutation(np.resize(levels, k // 512 * 4)).reshape(k // 512, 4)
    idx = np.arange(k)
    return np.exp2(a[idx // 512, idx % 128 // 32])


BF16 = ml_dtypes.bfloat16


def bf(x):
    return np.asarray(x, np.float32).astype(BF16)


def f64(x):
    return np.asarray(x).astype(np.float64)


E2M1 = np.array([0.0, 0.5, 1.0, 1.5, 2.0, 3.0, 4.0, 6.0, -0.0, -0.5, -1.0, -1.5, -2.0, -3.0, -4.0, -6.0])


def pack_weight(w, fmt):
    k, n = w.shape
    w = f64(bf(w)).reshape(k // 32, 32, n)
    amax = np.abs(w).max(1)
    if fmt == "e4m3":
        byte = np.frexp(amax)[1] - 1 + 127 - 7
    else:
        mant, ex = np.frexp(amax / 6.0)
        byte = np.where(mant > 0.5, ex, ex - 1) + 127
    byte = np.clip(np.where(amax > 0, byte, 1), 1, 254)
    scaled = (w * np.exp2(127.0 - byte)[:, None, :]).reshape(k, n).astype(np.float32)
    by_word = np.ascontiguousarray(scaled.reshape(k // 512, 128, 4, n).transpose(0, 1, 3, 2))
    if fmt == "e4m3":
        words = by_word.astype(ml_dtypes.float8_e4m3fn).view(np.uint8)
    else:
        c = by_word.astype(ml_dtypes.float4_e2m1fn).view(np.uint8) & 0xF
        words = c[..., 0::2] | (c[..., 1::2] << 4)
    return np.ascontiguousarray(words), np.ascontiguousarray(byte.astype(np.uint8).reshape(k // 512, 16, n))


def unpack_weight(words, scales, fmt):
    g, p, n, _ = words.shape
    if fmt == "e4m3":
        vals = np.ascontiguousarray(words).view(ml_dtypes.float8_e4m3fn).astype(np.float64)
    else:
        nib = np.empty((g, p, n, 4), np.uint8)
        nib[..., 0::2] = words & 0xF
        nib[..., 1::2] = words >> 4
        vals = E2M1[nib]
    vals = vals * np.repeat(np.exp2(scales.astype(np.float64) - 127.0), 8, axis=1)[..., None]
    return vals.transpose(0, 1, 3, 2).reshape(g * 512, n)


B, EN_MID, DE_MID = 1024, 2048, 4096
K1 = EN_MID // 2
K2 = DE_MID // 2


def setup_inputs():
    s = mx_kscale(K1)
    in_data = np.random.standard_normal((B, K1, 2)) * s[None, :, None]
    w = np.random.standard_normal((DE_MID, K1)) / np.sqrt(K1) / s[None, :]
    W_words, W_scales = pack_weight(w.T, "e4m3")
    return {"in_data": bf(in_data.reshape(B, EN_MID)),
            "W_words": W_words,
            "W_scales": W_scales,
            "bias": bf(np.random.standard_normal(DE_MID) * 0.25)}


def reference(in_data, W_words, W_scales, bias):
    Bsz = in_data.shape[0]
    x_imag = f64(in_data).reshape(Bsz, K1, 2)[:, :, 1]
    tmp = mxq(x_imag, 1, "e4m3") @ unpack_weight(W_words, W_scales, "e4m3")
    act = np.maximum(tmp + f64(bias), 0.0)
    out_r = act[:, :K2] - act[:, K2:]
    out = np.stack([out_r, np.zeros_like(out_r)], axis=2)
    return out.reshape(Bsz, DE_MID, 1)

@@ -1,0 +1,235 @@
+from contextlib import ExitStack
+
+import concourse.mybir as mybir
+from concourse.masks import make_identity
+
+F32 = mybir.dt.float32
+BF16 = mybir.dt.bfloat16
+I32 = mybir.dt.int32
+U32 = mybir.dt.uint32
+U8 = mybir.dt.uint8
+FP8X4 = mybir.dt.float8_e4m3fn_x4
+ALU = mybir.AluOpType
+
+P = 128
+B = 1024
+K = 1024
+N = 4096
+J = N // 2
+PASSES = K // (4 * P)
+B_TILES = B // P
+B_RUN = 512
+RUN_TILES = B_RUN // P
+RUNS = B // B_RUN
+J_TILES = J // P
+PAIR = 2
+ROUNDS_PER_RUN = J_TILES // PAIR
+ROUNDS = RUNS * ROUNDS_PER_RUN
+W_CHUNKS = 4
+STORE_ROUNDS = 2
+
+FLOPS = 2 * B * K * N
+
+
+def tile_middlelayer_kernel(tc, in_data, W_words, W_scales, bias, out):
+    nc = tc.nc
+    out_rows = out.rearrange("b n o -> b (n o)")
+
+    with ExitStack() as ctx:
+        ctx.enter_context(tc.manual_schedule())
+        keep = ctx.enter_context(tc.tile_pool(name="keep", bufs=1))
+        x_stage = ctx.enter_context(tc.tile_pool(name="x_stage", bufs=3))
+        fold = ctx.enter_context(tc.tile_pool(name="fold", bufs=3))
+        folded = ctx.enter_context(tc.tile_pool(name="folded", bufs=3 * PAIR))
+        rows_out = ctx.enter_context(tc.tile_pool(name="rows_out", bufs=3 * RUN_TILES))
+        products = ctx.enter_context(tc.psum_pool(name="products", bufs=4))
+        turned = ctx.enter_context(tc.psum_pool(name="turned", bufs=1))
+
+        x_raw = [keep.tile([P, 2 * K], BF16, name="x_raw%d" % bt) for bt in range(B_TILES)]
+        x_codes = keep.tile([P, PASSES, B], U32, name="x_codes", align_bytes=64)
+        x_scales = keep.tile([P, PASSES, B], U8, name="x_scales", align_bytes=64)
+        w_codes = keep.tile([P, PASSES, N], U32, name="w_codes", align_bytes=64)
+        w_scales = keep.tile([P, PASSES, N], U8, name="w_scales", align_bytes=64)
+        identity = keep.tile([P, P], F32, name="identity")
+        zeros = keep.tile([P, 2 * P], BF16, name="zeros")
+        bias_rows = keep.tile([P, P], BF16, name="bias_rows")
+        bias_rows_f32 = keep.tile([P, P], F32, name="bias_rows_f32")
+        neg_b1 = keep.tile([P, J_TILES], F32, name="neg_b1")
+        b2_minus_b1 = keep.tile([P, J_TILES], F32, name="b2_minus_b1")
+
+        def load_x(bt):
+            nc.sync.dma_start(out=x_raw[bt][:], in_=in_data[bt * P : (bt + 1) * P, :])
+
+        nc.vector.memset(bias_rows[:], 0.0)
+        nc.scalar.dma_start(out=bias_rows[0 : N // P, :], in_=bias.rearrange("(r c) -> r c", c=P))
+        for bt in range(RUN_TILES):
+            load_x(bt)
+        nc.vector.memset(w_scales[:].bitcast(I32), 0)
+        for g in range(PASSES):
+            for low in range(8):
+                first = 32 * (low // 4) + low % 4
+                nc.sync.dma_start(
+                    out=w_scales[first:P:64, g, :].bitcast(I32),
+                    in_=W_scales[g, low:16:8, :].bitcast(I32),
+                )
+        chunk = J // W_CHUNKS
+        for c in range(W_CHUNKS):
+            for g in range(PASSES):
+                words = W_words[g].rearrange("p n t -> p (n t)").bitcast(I32)
+                nc.sync.dma_start(
+                    out=w_codes[:, g, :]
+                    .bitcast(I32)
+                    .rearrange("p (s n) -> p s n", s=2)[:, :, c * chunk : (c + 1) * chunk],
+                    in_=words.rearrange("p (s n) -> p s n", s=2)[:, :, c * chunk : (c + 1) * chunk],
+                )
+        for bt in range(RUN_TILES, B_TILES):
+            load_x(bt)
+
+        make_identity(nc, identity[:])
+        nc.vector.memset(zeros[:], 0.0)
+        turned_banks = [turned.tile([P, 4 * P], F32, name="turned%d" % q) for q in range(RUN_TILES)]
+        for q in range(RUN_TILES):
+            nc.tensor.matmul(
+                out=turned_banks[q][:, 2 * P : 4 * P],
+                lhsT=zeros[:, 0:P],
+                rhs=zeros[:],
+                start=True,
+                stop=True,
+            )
+        nc.vector.tensor_copy(out=bias_rows_f32[:], in_=bias_rows[:])
+        bias_cols = products.tile([P, B_RUN], F32, name="bias_cols", tag="bank")
+        nc.tensor.transpose(out=bias_cols[:, 0:P], in_=bias_rows_f32[:], identity=identity[:])
+        nc.vector.tensor_scalar(
+            out=neg_b1[:], in0=bias_cols[:, 0:J_TILES], scalar1=-1.0, scalar2=None, op0=ALU.mult
+        )
+        nc.vector.tensor_tensor(
+            out=b2_minus_b1[:], in0=bias_cols[:, J_TILES : 2 * J_TILES], in1=neg_b1[:], op=ALU.add
+        )
+
+        def take_imaginary(bt):
+            x_imag = x_stage.tile([P, PASSES, 2, P, 2], BF16, name="x_imag")
+            pairs = x_raw[bt][:].rearrange(
+                "b (g p u e c) -> b g u p e c", g=PASSES, p=P, u=2, e=2, c=2
+            )
+            for g in range(PASSES):
+                nc.vector.tensor_copy(out=x_imag[:, g], in_=pairs[:, g, :, :, :, 1])
+            return x_imag
+
+        def transpose_x(x_imag):
+            words = x_imag[:].rearrange("b g u p e -> b (g u p e)").bitcast(F32)
+            x_turned = products.tile([P, B_RUN], F32, name="x_turned", tag="bank")
+            for gu in range(2 * PASSES):
+                cols = slice(gu * P, (gu + 1) * P)
+                nc.tensor.transpose(out=x_turned[:, cols], in_=words[:, cols], identity=identity[:])
+            grouped = x_stage.tile([P, PASSES, P, 4], BF16, name="grouped", align_bytes=64)
+            nc.scalar.copy(
+                out=grouped[:]
+                .rearrange("p g b t -> p g (b t)")
+                .bitcast(F32)
+                .rearrange("p g (b u) -> p g b u", u=2),
+                in_=x_turned[:].rearrange("p (g u b) -> p g b u", g=PASSES, u=2),
+            )
+            return grouped
+
+        def quantise_x(bt, grouped):
+            rows = slice(bt * P, (bt + 1) * P)
+            for g in range(PASSES):
+                nc.vector.quantize_mx(
+                    out=x_codes[:, g, rows].bitcast(FP8X4),
+                    scales=x_scales[:, g, rows],
+                    in_=grouped[:, g].rearrange("p b t -> p (b t)"),
+                )
+
+        def product(n_tile, run):
+            bank = products.tile([P, B_RUN], F32, name="product", tag="bank")
+            n_cols = slice(n_tile * P, (n_tile + 1) * P)
+            b_cols = slice(run * B_RUN, (run + 1) * B_RUN)
+            for g in range(PASSES):
+                nc.tensor.matmul_mx(
+                    out=bank[:],
+                    lhsT=w_codes[:, g, n_cols].bitcast(FP8X4),
+                    lhsT_scale=w_scales[:, g, n_cols],
+                    rhs=x_codes[:, g, b_cols].bitcast(FP8X4),
+                    rhs_scale=x_scales[:, g, b_cols],
+                    start=(g == 0),
+                    stop=(g == PASSES - 1),
+                )
+            return bank
+
+        def multiply_and_fold(rnd):
+            run, pair = divmod(rnd, ROUNDS_PER_RUN)
+            r_tiles = []
+            for a in range(PAIR):
+                jt = pair * PAIR + a
+                p2 = product(J_TILES + jt, run)
+                p1 = product(jt, run)
+                relu2 = fold.tile([P, B_RUN], F32, name="relu2")
+                nc.vector.tensor_scalar(
+                    out=relu2[:],
+                    in0=p2[:],
+                    scalar1=b2_minus_b1[:, jt : jt + 1],
+                    scalar2=neg_b1[:, jt : jt + 1],
+                    op0=ALU.add,
+                    op1=ALU.max,
+                )
+                r_tile = folded.tile([P, B_RUN], F32, name="r_tile")
+                nc.vector.scalar_tensor_tensor(
+                    out=r_tile[:],
+                    in0=p1[:],
+                    scalar=neg_b1[:, jt : jt + 1],
+                    in1=relu2[:],
+                    op0=ALU.max,
+                    op1=ALU.subtract,
+                )
+                r_tiles.append(r_tile)
+            return r_tiles
+
+        def turn_and_store(rnd, r_tiles, rows):
+            run, pair = divmod(rnd, ROUNDS_PER_RUN)
+            part = pair % STORE_ROUNDS
+            width = 2 * PAIR * P
+            for q in range(RUN_TILES):
+                bank = turned_banks[q]
+                for a in range(PAIR):
+                    nc.tensor.transpose(
+                        out=bank[:, a * P : (a + 1) * P],
+                        in_=r_tiles[a][:, q * P : (q + 1) * P],
+                        identity=identity[:],
+                    )
+                if part == 0:
+                    rows[q] = rows_out.tile([P, STORE_ROUNDS * width], F32, name="rows")
+                nc.scalar.copy(
+                    out=rows[q][:, part * width : (part + 1) * width].rearrange(
+                        "p (c e) -> p c e", e=2
+                    ),
+                    in_=bank[:].rearrange("p (e c) -> p c e", e=2),
+                )
+                if part == STORE_ROUNDS - 1:
+                    bt = run * RUN_TILES + q
+                    first = (pair - part) * width
+                    nc.sync.dma_start(
+                        out=out_rows[bt * P : (bt + 1) * P, first : first + STORE_ROUNDS * width],
+                        in_=rows[q][:],
+                    )
+
+        grouped_tiles = {}
+        for bt in range(RUN_TILES + 1):
+            if bt < RUN_TILES:
+                grouped_tiles[bt] = transpose_x(take_imaginary(bt))
+            if bt >= 1:
+                quantise_x(bt - 1, grouped_tiles[bt - 1])
+
+        rows = {}
+        r_tiles = {}
+        for rnd in range(ROUNDS + 1):
+            prepares_x = RUN_TILES <= rnd < B_TILES
+            if prepares_x:
+                x_imag = take_imaginary(rnd)
+            if rnd < ROUNDS:
+                r_tiles[rnd] = multiply_and_fold(rnd)
+            if prepares_x:
+                grouped_tiles[rnd] = transpose_x(x_imag)
+            if rnd >= 1:
+                turn_and_store(rnd - 1, r_tiles[rnd - 1], rows)
+            if prepares_x:
+                quantise_x(rnd, grouped_tiles[rnd])

@@ -45,7 +45,7 @@ def tile_middlelayer_kernel(tc, in_data, W_words, W_scales, bias, out):
         products = ctx.enter_context(tc.psum_pool(name="products", bufs=4))
         turned = ctx.enter_context(tc.psum_pool(name="turned", bufs=1))
 
-        x_raw = [keep.tile([P, 2 * K], BF16, name="x_raw%d" % bt) for bt in range(B_TILES)]
+        x_raw = [keep.tile([P, 2, 2 * K], BF16, name="x_raw%d" % i) for i in range(B_TILES // 2)]
         x_codes = keep.tile([P, PASSES, B], U32, name="x_codes", align_bytes=64)
         x_scales = keep.tile([P, PASSES, B], U8, name="x_scales", align_bytes=64)
         w_codes = keep.tile([P, PASSES, N], U32, name="w_codes", align_bytes=64)
@@ -57,21 +57,22 @@ def tile_middlelayer_kernel(tc, in_data, W_words, W_scales, bias, out):
         neg_b1 = keep.tile([P, J_TILES], F32, name="neg_b1")
         b2_minus_b1 = keep.tile([P, J_TILES], F32, name="b2_minus_b1")
 
-        def load_x(bt):
-            nc.sync.dma_start(out=x_raw[bt][:], in_=in_data[bt * P : (bt + 1) * P, :])
+        def load_x(i):
+            nc.sync.dma_start(
+                out=x_raw[i][:],
+                in_=in_data[2 * i * P : 2 * (i + 1) * P, :].rearrange("(t p) c -> p t c", p=P),
+            )
 
         nc.vector.memset(bias_rows[:], 0.0)
         nc.scalar.dma_start(out=bias_rows[0 : N // P, :], in_=bias.rearrange("(r c) -> r c", c=P))
-        for bt in range(RUN_TILES):
-            load_x(bt)
+        for i in range(RUN_TILES // 2):
+            load_x(i)
         nc.vector.memset(w_scales[:].bitcast(I32), 0)
-        for g in range(PASSES):
-            for low in range(8):
-                first = 32 * (low // 4) + low % 4
-                nc.sync.dma_start(
-                    out=w_scales[first:P:64, g, :].bitcast(I32),
-                    in_=W_scales[g, low:16:8, :].bitcast(I32),
-                )
+        for r in range(4):
+            nc.sync.dma_start(
+                out=w_scales[r:P:32, :, :].bitcast(I32),
+                in_=W_scales[:, r:16:4, :].bitcast(I32).rearrange("g q n -> q g n"),
+            )
         chunk = J // W_CHUNKS
         for c in range(W_CHUNKS):
             for g in range(PASSES):
@@ -82,8 +83,8 @@ def tile_middlelayer_kernel(tc, in_data, W_words, W_scales, bias, out):
                     .rearrange("p (s n) -> p s n", s=2)[:, :, c * chunk : (c + 1) * chunk],
                     in_=words.rearrange("p (s n) -> p s n", s=2)[:, :, c * chunk : (c + 1) * chunk],
                 )
-        for bt in range(RUN_TILES, B_TILES):
-            load_x(bt)
+        for i in range(RUN_TILES // 2, B_TILES // 2):
+            load_x(i)
 
         make_identity(nc, identity[:])
         nc.vector.memset(zeros[:], 0.0)
@@ -108,7 +109,7 @@ def tile_middlelayer_kernel(tc, in_data, W_words, W_scales, bias, out):
 
         def take_imaginary(bt):
             x_imag = x_stage.tile([P, PASSES, 2, P, 2], BF16, name="x_imag")
-            pairs = x_raw[bt][:].rearrange(
+            pairs = x_raw[bt // 2][:, bt % 2, :].rearrange(
                 "b (g p u e c) -> b g u p e c", g=PASSES, p=P, u=2, e=2, c=2
             )
             for g in range(PASSES):
@@ -188,6 +189,7 @@ def tile_middlelayer_kernel(tc, in_data, W_words, W_scales, bias, out):
             run, pair = divmod(rnd, ROUNDS_PER_RUN)
             part = pair % STORE_ROUNDS
             width = 2 * PAIR * P
+            copy_out = nc.vector.tensor_copy if rnd == ROUNDS - 1 else nc.scalar.copy
             for q in range(RUN_TILES):
                 bank = turned_banks[q]
                 for a in range(PAIR):
@@ -198,7 +200,7 @@ def tile_middlelayer_kernel(tc, in_data, W_words, W_scales, bias, out):
                     )
                 if part == 0:
                     rows[q] = rows_out.tile([P, STORE_ROUNDS * width], F32, name="rows")
-                nc.scalar.copy(
+                copy_out(
                     out=rows[q][:, part * width : (part + 1) * width].rearrange(
                         "p (c e) -> p c e", e=2
                     ),

@@ -26,7 +26,6 @@ PAIR = 2
 ROUNDS_PER_RUN = J_TILES // PAIR
 ROUNDS = RUNS * ROUNDS_PER_RUN
 W_CHUNKS = 4
-STORE_ROUNDS = 2
 
 FLOPS = 2 * B * K * N
 
@@ -41,11 +40,11 @@ def tile_middlelayer_kernel(tc, in_data, W_words, W_scales, bias, out):
         x_stage = ctx.enter_context(tc.tile_pool(name="x_stage", bufs=3))
         fold = ctx.enter_context(tc.tile_pool(name="fold", bufs=3))
         folded = ctx.enter_context(tc.tile_pool(name="folded", bufs=3 * PAIR))
-        rows_out = ctx.enter_context(tc.tile_pool(name="rows_out", bufs=3 * RUN_TILES))
+        rows_out = ctx.enter_context(tc.tile_pool(name="rows_out", bufs=4 * RUN_TILES))
         products = ctx.enter_context(tc.psum_pool(name="products", bufs=4))
         turned = ctx.enter_context(tc.psum_pool(name="turned", bufs=1))
 
-        x_raw = [keep.tile([P, 2, 2 * K], BF16, name="x_raw%d" % i) for i in range(B_TILES // 2)]
+        x_raw = [keep.tile([P, 2 * K], BF16, name="x_raw%d" % bt) for bt in range(B_TILES)]
         x_codes = keep.tile([P, PASSES, B], U32, name="x_codes", align_bytes=64)
         x_scales = keep.tile([P, PASSES, B], U8, name="x_scales", align_bytes=64)
         w_codes = keep.tile([P, PASSES, N], U32, name="w_codes", align_bytes=64)
@@ -57,16 +56,13 @@ def tile_middlelayer_kernel(tc, in_data, W_words, W_scales, bias, out):
         neg_b1 = keep.tile([P, J_TILES], F32, name="neg_b1")
         b2_minus_b1 = keep.tile([P, J_TILES], F32, name="b2_minus_b1")
 
-        def load_x(i):
-            nc.sync.dma_start(
-                out=x_raw[i][:],
-                in_=in_data[2 * i * P : 2 * (i + 1) * P, :].rearrange("(t p) c -> p t c", p=P),
-            )
+        def load_x(bt):
+            nc.sync.dma_start(out=x_raw[bt][:], in_=in_data[bt * P : (bt + 1) * P, :])
 
         nc.vector.memset(bias_rows[:], 0.0)
         nc.scalar.dma_start(out=bias_rows[0 : N // P, :], in_=bias.rearrange("(r c) -> r c", c=P))
-        for i in range(RUN_TILES // 2):
-            load_x(i)
+        for bt in range(RUN_TILES):
+            load_x(bt)
         nc.vector.memset(w_scales[:].bitcast(I32), 0)
         for r in range(4):
             nc.sync.dma_start(
@@ -83,8 +79,8 @@ def tile_middlelayer_kernel(tc, in_data, W_words, W_scales, bias, out):
                     .rearrange("p (s n) -> p s n", s=2)[:, :, c * chunk : (c + 1) * chunk],
                     in_=words.rearrange("p (s n) -> p s n", s=2)[:, :, c * chunk : (c + 1) * chunk],
                 )
-        for i in range(RUN_TILES // 2, B_TILES // 2):
-            load_x(i)
+        for bt in range(RUN_TILES, B_TILES):
+            load_x(bt)
 
         make_identity(nc, identity[:])
         nc.vector.memset(zeros[:], 0.0)
@@ -109,7 +105,7 @@ def tile_middlelayer_kernel(tc, in_data, W_words, W_scales, bias, out):
 
         def take_imaginary(bt):
             x_imag = x_stage.tile([P, PASSES, 2, P, 2], BF16, name="x_imag")
-            pairs = x_raw[bt // 2][:, bt % 2, :].rearrange(
+            pairs = x_raw[bt][:].rearrange(
                 "b (g p u e c) -> b g u p e c", g=PASSES, p=P, u=2, e=2, c=2
             )
             for g in range(PASSES):
@@ -157,39 +153,34 @@ def tile_middlelayer_kernel(tc, in_data, W_words, W_scales, bias, out):
                 )
             return bank
 
-        def multiply_and_fold(rnd):
+        def multiply_and_fold(rnd, a):
             run, pair = divmod(rnd, ROUNDS_PER_RUN)
-            r_tiles = []
-            for a in range(PAIR):
-                jt = pair * PAIR + a
-                p2 = product(J_TILES + jt, run)
-                p1 = product(jt, run)
-                relu2 = fold.tile([P, B_RUN], F32, name="relu2")
-                nc.vector.tensor_scalar(
-                    out=relu2[:],
-                    in0=p2[:],
-                    scalar1=b2_minus_b1[:, jt : jt + 1],
-                    scalar2=neg_b1[:, jt : jt + 1],
-                    op0=ALU.add,
-                    op1=ALU.max,
-                )
-                r_tile = folded.tile([P, B_RUN], F32, name="r_tile")
-                nc.vector.scalar_tensor_tensor(
-                    out=r_tile[:],
-                    in0=p1[:],
-                    scalar=neg_b1[:, jt : jt + 1],
-                    in1=relu2[:],
-                    op0=ALU.max,
-                    op1=ALU.subtract,
-                )
-                r_tiles.append(r_tile)
-            return r_tiles
+            jt = pair * PAIR + a
+            p2 = product(J_TILES + jt, run)
+            p1 = product(jt, run)
+            relu2 = fold.tile([P, B_RUN], F32, name="relu2")
+            nc.vector.tensor_scalar(
+                out=relu2[:],
+                in0=p2[:],
+                scalar1=b2_minus_b1[:, jt : jt + 1],
+                scalar2=neg_b1[:, jt : jt + 1],
+                op0=ALU.add,
+                op1=ALU.max,
+            )
+            r_tile = folded.tile([P, B_RUN], F32, name="r_tile")
+            nc.vector.scalar_tensor_tensor(
+                out=r_tile[:],
+                in0=p1[:],
+                scalar=neg_b1[:, jt : jt + 1],
+                in1=relu2[:],
+                op0=ALU.max,
+                op1=ALU.subtract,
+            )
+            return r_tile
 
-        def turn_and_store(rnd, r_tiles, rows):
+        def turn_and_store(rnd, r_tiles):
             run, pair = divmod(rnd, ROUNDS_PER_RUN)
-            part = pair % STORE_ROUNDS
             width = 2 * PAIR * P
-            copy_out = nc.vector.tensor_copy if rnd == ROUNDS - 1 else nc.scalar.copy
             for q in range(RUN_TILES):
                 bank = turned_banks[q]
                 for a in range(PAIR):
@@ -198,21 +189,17 @@ def tile_middlelayer_kernel(tc, in_data, W_words, W_scales, bias, out):
                         in_=r_tiles[a][:, q * P : (q + 1) * P],
                         identity=identity[:],
                     )
-                if part == 0:
-                    rows[q] = rows_out.tile([P, STORE_ROUNDS * width], F32, name="rows")
+                copy_out = nc.vector.tensor_copy if rnd == ROUNDS - 1 else nc.scalar.copy
+                rows = rows_out.tile([P, width], F32, name="rows")
                 copy_out(
-                    out=rows[q][:, part * width : (part + 1) * width].rearrange(
-                        "p (c e) -> p c e", e=2
-                    ),
+                    out=rows[:].rearrange("p (c e) -> p c e", e=2),
                     in_=bank[:].rearrange("p (e c) -> p c e", e=2),
                 )
-                if part == STORE_ROUNDS - 1:
-                    bt = run * RUN_TILES + q
-                    first = (pair - part) * width
-                    nc.sync.dma_start(
-                        out=out_rows[bt * P : (bt + 1) * P, first : first + STORE_ROUNDS * width],
-                        in_=rows[q][:],
-                    )
+                bt = run * RUN_TILES + q
+                nc.sync.dma_start(
+                    out=out_rows[bt * P : (bt + 1) * P, pair * width : (pair + 1) * width],
+                    in_=rows[:],
+                )
 
         grouped_tiles = {}
         for bt in range(RUN_TILES + 1):
@@ -221,17 +208,16 @@ def tile_middlelayer_kernel(tc, in_data, W_words, W_scales, bias, out):
             if bt >= 1:
                 quantise_x(bt - 1, grouped_tiles[bt - 1])
 
-        rows = {}
         r_tiles = {}
         for rnd in range(ROUNDS + 1):
             prepares_x = RUN_TILES <= rnd < B_TILES
             if prepares_x:
                 x_imag = take_imaginary(rnd)
             if rnd < ROUNDS:
-                r_tiles[rnd] = multiply_and_fold(rnd)
+                r_tiles[rnd] = [multiply_and_fold(rnd, a) for a in range(PAIR)]
             if prepares_x:
                 grouped_tiles[rnd] = transpose_x(x_imag)
             if rnd >= 1:
-                turn_and_store(rnd - 1, r_tiles[rnd - 1], rows)
+                turn_and_store(rnd - 1, r_tiles[rnd - 1])
             if prepares_x:
                 quantise_x(rnd, grouped_tiles[rnd])

@@ -25,7 +25,7 @@ J_TILES = J // P
 PAIR = 2
 ROUNDS_PER_RUN = J_TILES // PAIR
 ROUNDS = RUNS * ROUNDS_PER_RUN
-W_CHUNKS = 4
+W_CHUNK_TILES = (2, 2, 4, 4, 4)
 
 FLOPS = 2 * B * K * N
 
@@ -48,7 +48,7 @@ def tile_middlelayer_kernel(tc, in_data, W_words, W_scales, bias, out):
         x_codes = keep.tile([P, PASSES, B], U32, name="x_codes", align_bytes=64)
         x_scales = keep.tile([P, PASSES, B], U8, name="x_scales", align_bytes=64)
         w_codes = keep.tile([P, PASSES, N], U32, name="w_codes", align_bytes=64)
-        w_scales = keep.tile([P, PASSES, N], U8, name="w_scales", align_bytes=64)
+        w_scales = keep.tile([P, N], U8, name="w_scales", align_bytes=64)
         identity = keep.tile([P, P], F32, name="identity")
         zeros = keep.tile([P, 2 * P], BF16, name="zeros")
         bias_rows = keep.tile([P, P], BF16, name="bias_rows")
@@ -64,20 +64,20 @@ def tile_middlelayer_kernel(tc, in_data, W_words, W_scales, bias, out):
         for bt in range(RUN_TILES):
             load_x(bt)
         nc.vector.memset(w_scales[:].bitcast(I32), 0)
-        for r in range(4):
+        for quadrant in range(4):
             nc.sync.dma_start(
-                out=w_scales[r:P:32, :, :].bitcast(I32),
-                in_=W_scales[:, r:16:4, :].bitcast(I32).rearrange("g q n -> q g n"),
+                out=w_scales[32 * quadrant : 32 * quadrant + 4 * PASSES, :].bitcast(I32),
+                in_=W_scales[:, 4 * quadrant : 4 * quadrant + 4, :].bitcast(I32),
             )
-        chunk = J // W_CHUNKS
-        for c in range(W_CHUNKS):
+        first_tile = 0
+        for tiles in W_CHUNK_TILES:
+            cols = slice(first_tile * P, (first_tile + tiles) * P)
+            first_tile += tiles
             for g in range(PASSES):
                 words = W_words[g].rearrange("p n t -> p (n t)").bitcast(I32)
                 nc.sync.dma_start(
-                    out=w_codes[:, g, :]
-                    .bitcast(I32)
-                    .rearrange("p (s n) -> p s n", s=2)[:, :, c * chunk : (c + 1) * chunk],
-                    in_=words.rearrange("p (s n) -> p s n", s=2)[:, :, c * chunk : (c + 1) * chunk],
+                    out=w_codes[:, g, :].bitcast(I32).rearrange("p (s n) -> p s n", s=2)[:, :, cols],
+                    in_=words.rearrange("p (s n) -> p s n", s=2)[:, :, cols],
                 )
         for bt in range(RUN_TILES, B_TILES):
             load_x(bt)
@@ -145,7 +145,7 @@ def tile_middlelayer_kernel(tc, in_data, W_words, W_scales, bias, out):
                 nc.tensor.matmul_mx(
                     out=bank[:],
                     lhsT=w_codes[:, g, n_cols].bitcast(FP8X4),
-                    lhsT_scale=w_scales[:, g, n_cols],
+                    lhsT_scale=w_scales[4 * g : P, n_cols],
                     rhs=x_codes[:, g, b_cols].bitcast(FP8X4),
                     rhs_scale=x_scales[:, g, b_cols],
                     start=(g == 0),

@@ -38,7 +38,7 @@ def tile_middlelayer_kernel(tc, in_data, W_words, W_scales, bias, out):
         ctx.enter_context(tc.manual_schedule())
         keep = ctx.enter_context(tc.tile_pool(name="keep", bufs=1))
         x_stage = ctx.enter_context(tc.tile_pool(name="x_stage", bufs=3))
-        fold = ctx.enter_context(tc.tile_pool(name="fold", bufs=3))
+        fold = ctx.enter_context(tc.tile_pool(name="fold", bufs=2 * PAIR))
         folded = ctx.enter_context(tc.tile_pool(name="folded", bufs=3 * PAIR))
         rows_out = ctx.enter_context(tc.tile_pool(name="rows_out", bufs=4 * RUN_TILES))
         products = ctx.enter_context(tc.psum_pool(name="products", bufs=4))
@@ -108,8 +108,8 @@ def tile_middlelayer_kernel(tc, in_data, W_words, W_scales, bias, out):
             pairs = x_raw[bt][:].rearrange(
                 "b (g p u e c) -> b g u p e c", g=PASSES, p=P, u=2, e=2, c=2
             )
-            for g in range(PASSES):
-                nc.vector.tensor_copy(out=x_imag[:, g], in_=pairs[:, g, :, :, :, 1])
+            nc.vector.tensor_copy(out=x_imag[:, 0], in_=pairs[:, 0, :, :, :, 1])
+            nc.scalar.copy(out=x_imag[:, 1], in_=pairs[:, 1, :, :, :, 1])
             return x_imag
 
         def transpose_x(x_imag):
@@ -153,30 +153,34 @@ def tile_middlelayer_kernel(tc, in_data, W_words, W_scales, bias, out):
                 )
             return bank
 
-        def multiply_and_fold(rnd, a):
+        def multiply_and_fold(rnd):
             run, pair = divmod(rnd, ROUNDS_PER_RUN)
-            jt = pair * PAIR + a
-            p2 = product(J_TILES + jt, run)
-            p1 = product(jt, run)
-            relu2 = fold.tile([P, B_RUN], F32, name="relu2")
-            nc.vector.tensor_scalar(
-                out=relu2[:],
-                in0=p2[:],
-                scalar1=b2_minus_b1[:, jt : jt + 1],
-                scalar2=neg_b1[:, jt : jt + 1],
-                op0=ALU.add,
-                op1=ALU.max,
-            )
-            r_tile = folded.tile([P, B_RUN], F32, name="r_tile")
-            nc.vector.scalar_tensor_tensor(
-                out=r_tile[:],
-                in0=p1[:],
-                scalar=neg_b1[:, jt : jt + 1],
-                in1=relu2[:],
-                op0=ALU.max,
-                op1=ALU.subtract,
-            )
-            return r_tile
+            tiles = [pair * PAIR + a for a in range(PAIR)]
+            p2 = [product(J_TILES + jt, run) for jt in tiles]
+            p1 = [product(jt, run) for jt in tiles]
+            relu2 = []
+            for a, jt in enumerate(tiles):
+                relu2.append(fold.tile([P, B_RUN], F32, name="relu2"))
+                nc.vector.tensor_scalar(
+                    out=relu2[a][:],
+                    in0=p2[a][:],
+                    scalar1=b2_minus_b1[:, jt : jt + 1],
+                    scalar2=neg_b1[:, jt : jt + 1],
+                    op0=ALU.add,
+                    op1=ALU.max,
+                )
+            r_tiles = []
+            for a, jt in enumerate(tiles):
+                r_tiles.append(folded.tile([P, B_RUN], F32, name="r_tile"))
+                nc.vector.scalar_tensor_tensor(
+                    out=r_tiles[a][:],
+                    in0=p1[a][:],
+                    scalar=neg_b1[:, jt : jt + 1],
+                    in1=relu2[a][:],
+                    op0=ALU.max,
+                    op1=ALU.subtract,
+                )
+            return r_tiles
 
         def turn_and_store(rnd, r_tiles):
             run, pair = divmod(rnd, ROUNDS_PER_RUN)
@@ -202,11 +206,14 @@ def tile_middlelayer_kernel(tc, in_data, W_words, W_scales, bias, out):
                 )
 
         grouped_tiles = {}
-        for bt in range(RUN_TILES + 1):
-            if bt < RUN_TILES:
-                grouped_tiles[bt] = transpose_x(take_imaginary(bt))
+        x_imags = {0: take_imaginary(0)}
+        for bt in range(RUN_TILES):
+            if bt + 1 < RUN_TILES:
+                x_imags[bt + 1] = take_imaginary(bt + 1)
+            grouped_tiles[bt] = transpose_x(x_imags[bt])
             if bt >= 1:
                 quantise_x(bt - 1, grouped_tiles[bt - 1])
+        quantise_x(RUN_TILES - 1, grouped_tiles[RUN_TILES - 1])
 
         r_tiles = {}
         for rnd in range(ROUNDS + 1):
@@ -214,7 +221,7 @@ def tile_middlelayer_kernel(tc, in_data, W_words, W_scales, bias, out):
             if prepares_x:
                 x_imag = take_imaginary(rnd)
             if rnd < ROUNDS:
-                r_tiles[rnd] = [multiply_and_fold(rnd, a) for a in range(PAIR)]
+                r_tiles[rnd] = multiply_and_fold(rnd)
             if prepares_x:
                 grouped_tiles[rnd] = transpose_x(x_imag)
             if rnd >= 1:

@@ -10,6 +10,7 @@ U32 = mybir.dt.uint32
 U8 = mybir.dt.uint8
 FP8X4 = mybir.dt.float8_e4m3fn_x4
 ALU = mybir.AluOpType
+ACT = mybir.ActivationFunctionType
 
 P = 128
 B = 1024
@@ -18,14 +19,12 @@ N = 4096
 J = N // 2
 PASSES = K // (4 * P)
 B_TILES = B // P
-B_RUN = 512
-RUN_TILES = B_RUN // P
-RUNS = B // B_RUN
 J_TILES = J // P
-PAIR = 2
-ROUNDS_PER_RUN = J_TILES // PAIR
-ROUNDS = RUNS * ROUNDS_PER_RUN
-W_CHUNK_TILES = (2, 2, 4, 4, 4)
+BANK = 512
+JX = 1536
+JX_TILES = JX // P
+CHUNKS = (J - JX) // BANK
+WIDE_ROWS = 4
 
 FLOPS = 2 * B * K * N
 
@@ -38,9 +37,11 @@ def tile_middlelayer_kernel(tc, in_data, W_words, W_scales, bias, out):
         ctx.enter_context(tc.manual_schedule())
         keep = ctx.enter_context(tc.tile_pool(name="keep", bufs=1))
         x_stage = ctx.enter_context(tc.tile_pool(name="x_stage", bufs=3))
-        fold = ctx.enter_context(tc.tile_pool(name="fold", bufs=2 * PAIR))
-        folded = ctx.enter_context(tc.tile_pool(name="folded", bufs=3 * PAIR))
-        rows_out = ctx.enter_context(tc.tile_pool(name="rows_out", bufs=4 * RUN_TILES))
+        fold = ctx.enter_context(tc.tile_pool(name="fold", bufs=4))
+        folded = ctx.enter_context(tc.tile_pool(name="folded", bufs=8))
+        rows_out = ctx.enter_context(tc.tile_pool(name="rows_out", bufs=16))
+        sums_pool = ctx.enter_context(tc.tile_pool(name="sums_pool", bufs=3))
+        acts_pool = ctx.enter_context(tc.tile_pool(name="acts_pool", bufs=5))
         products = ctx.enter_context(tc.psum_pool(name="products", bufs=4))
         turned = ctx.enter_context(tc.psum_pool(name="turned", bufs=1))
 
@@ -50,81 +51,99 @@ def tile_middlelayer_kernel(tc, in_data, W_words, W_scales, bias, out):
         w_codes = keep.tile([P, PASSES, N], U32, name="w_codes", align_bytes=64)
         w_scales = keep.tile([P, N], U8, name="w_scales", align_bytes=64)
         identity = keep.tile([P, P], F32, name="identity")
-        zeros = keep.tile([P, 2 * P], BF16, name="zeros")
+        zeros = keep.tile([P, 2 * BANK], BF16, name="zeros")
         bias_rows = keep.tile([P, P], BF16, name="bias_rows")
         bias_rows_f32 = keep.tile([P, P], F32, name="bias_rows_f32")
         neg_b1 = keep.tile([P, J_TILES], F32, name="neg_b1")
         b2_minus_b1 = keep.tile([P, J_TILES], F32, name="b2_minus_b1")
+        identity_bf16 = keep.tile([P, P], BF16, name="identity_bf16")
+        bias_all = keep.tile([P, 2, J - JX], F32, name="bias_all")
+        wide_rows = [keep.tile([P, 2 * BANK], F32, name="wide_rows%d" % i) for i in range(WIDE_ROWS)]
 
         def load_x(bt):
             nc.sync.dma_start(out=x_raw[bt][:], in_=in_data[bt * P : (bt + 1) * P, :])
 
-        nc.vector.memset(bias_rows[:], 0.0)
-        nc.scalar.dma_start(out=bias_rows[0 : N // P, :], in_=bias.rearrange("(r c) -> r c", c=P))
-        for bt in range(RUN_TILES):
-            load_x(bt)
-        nc.vector.memset(w_scales[:].bitcast(I32), 0)
-        for quadrant in range(4):
-            nc.sync.dma_start(
-                out=w_scales[32 * quadrant : 32 * quadrant + 4 * PASSES, :].bitcast(I32),
-                in_=W_scales[:, 4 * quadrant : 4 * quadrant + 4, :].bitcast(I32),
-            )
-        first_tile = 0
-        for tiles in W_CHUNK_TILES:
-            cols = slice(first_tile * P, (first_tile + tiles) * P)
-            first_tile += tiles
+        def load_w(j_from, j_to):
+            cols = slice(j_from * P, j_to * P)
             for g in range(PASSES):
                 words = W_words[g].rearrange("p n t -> p (n t)").bitcast(I32)
                 nc.sync.dma_start(
                     out=w_codes[:, g, :].bitcast(I32).rearrange("p (s n) -> p s n", s=2)[:, :, cols],
                     in_=words.rearrange("p (s n) -> p s n", s=2)[:, :, cols],
                 )
-        for bt in range(RUN_TILES, B_TILES):
+
+        nc.vector.memset(bias_rows[:], 0.0)
+        nc.scalar.dma_start(out=bias_rows[0 : N // P, :], in_=bias.rearrange("(r c) -> r c", c=P))
+        for bt in range(4):
             load_x(bt)
-
         make_identity(nc, identity[:])
-        nc.vector.memset(zeros[:], 0.0)
-        turned_banks = [turned.tile([P, 4 * P], F32, name="turned%d" % q) for q in range(RUN_TILES)]
-        for q in range(RUN_TILES):
-            nc.tensor.matmul(
-                out=turned_banks[q][:, 2 * P : 4 * P],
-                lhsT=zeros[:, 0:P],
-                rhs=zeros[:],
-                start=True,
-                stop=True,
+        make_identity(nc, identity_bf16[:])
+        nc.vector.memset(zeros[:].bitcast(I32), 0)
+        nc.vector.memset(w_scales[:].bitcast(I32), 0)
+        for rows in wide_rows[0:2]:
+            nc.scalar.copy(out=rows[:], in_=zeros[:])
+        for quadrant in range(4):
+            nc.sync.dma_start(
+                out=w_scales[32 * quadrant : 32 * quadrant + 4 * PASSES, :].bitcast(I32),
+                in_=W_scales[:, 4 * quadrant : 4 * quadrant + 4, :].bitcast(I32),
             )
-        nc.vector.tensor_copy(out=bias_rows_f32[:], in_=bias_rows[:])
-        bias_cols = products.tile([P, B_RUN], F32, name="bias_cols", tag="bank")
-        nc.tensor.transpose(out=bias_cols[:, 0:P], in_=bias_rows_f32[:], identity=identity[:])
-        nc.vector.tensor_scalar(
-            out=neg_b1[:], in0=bias_cols[:, 0:J_TILES], scalar1=-1.0, scalar2=None, op0=ALU.mult
-        )
-        nc.vector.tensor_tensor(
-            out=b2_minus_b1[:], in0=bias_cols[:, J_TILES : 2 * J_TILES], in1=neg_b1[:], op=ALU.add
-        )
+        load_w(0, 2)
+        load_w(2, 4)
+        load_w(4, 8)
+        load_w(8, 12)
+        for bt in range(4, B_TILES):
+            load_x(bt)
+        load_w(12, 16)
 
-        def take_imaginary(bt):
+        turned_banks = [turned.tile([P, BANK], F32, name="turned%d" % q) for q in range(4)]
+        for q in range(4):
+            nc.tensor.matmul(out=turned_banks[q][:, 2 * P : 4 * P], lhsT=zeros[:, 0:P], rhs=zeros[:, 0 : 2 * P], start=True, stop=True)
+
+        def bias_to_partitions():
+            nc.vector.tensor_copy(out=bias_rows_f32[:], in_=bias_rows[:])
+            bias_cols = products.tile([P, BANK], F32, name="bias_cols", tag="bank")
+            nc.tensor.transpose(out=bias_cols[:, 0:P], in_=bias_rows_f32[:], identity=identity[:])
+            nc.vector.tensor_scalar(out=neg_b1[:], in0=bias_cols[:, 0:J_TILES], scalar1=-1.0, scalar2=None, op0=ALU.mult)
+            nc.vector.tensor_tensor(out=b2_minus_b1[:], in0=bias_cols[:, J_TILES : 2 * J_TILES], in1=neg_b1[:], op=ALU.add)
+
+        def copy_on(engine, out_ap, in_ap):
+            if engine == "vector":
+                nc.vector.tensor_copy(out=out_ap, in_=in_ap)
+            else:
+                nc.scalar.copy(out=out_ap, in_=in_ap)
+
+        def spread_bias(s, c, engine):
+            bank = products.tile([P, BANK], F32, name="bias_bank", tag="bank")
+            cols = slice(c * BANK, (c + 1) * BANK)
+            for i in range(BANK // P):
+                row = (s * J + JX + c * BANK) // P + i
+                nc.tensor.matmul(
+                    out=bank[:, i * P : (i + 1) * P],
+                    lhsT=identity_bf16[:, row : row + 1].to_broadcast([P, P]),
+                    rhs=bias_rows[:],
+                    start=True,
+                    stop=True,
+                )
+            copy_on(engine, bias_all[:, s, cols], bank[:])
+
+        def take_imaginary(bt, engines):
             x_imag = x_stage.tile([P, PASSES, 2, P, 2], BF16, name="x_imag")
-            pairs = x_raw[bt][:].rearrange(
-                "b (g p u e c) -> b g u p e c", g=PASSES, p=P, u=2, e=2, c=2
-            )
-            nc.vector.tensor_copy(out=x_imag[:, 0], in_=pairs[:, 0, :, :, :, 1])
-            nc.scalar.copy(out=x_imag[:, 1], in_=pairs[:, 1, :, :, :, 1])
+            pairs = x_raw[bt][:].rearrange("b (g p u e c) -> b g u p e c", g=PASSES, p=P, u=2, e=2, c=2)
+            for g in range(PASSES):
+                copy_on(engines[g], x_imag[:, g], pairs[:, g, :, :, :, 1])
             return x_imag
 
-        def transpose_x(x_imag):
+        def transpose_x(x_imag, engine):
             words = x_imag[:].rearrange("b g u p e -> b (g u p e)").bitcast(F32)
-            x_turned = products.tile([P, B_RUN], F32, name="x_turned", tag="bank")
+            x_turned = products.tile([P, BANK], F32, name="x_turned", tag="bank")
             for gu in range(2 * PASSES):
                 cols = slice(gu * P, (gu + 1) * P)
                 nc.tensor.transpose(out=x_turned[:, cols], in_=words[:, cols], identity=identity[:])
             grouped = x_stage.tile([P, PASSES, P, 4], BF16, name="grouped", align_bytes=64)
-            nc.scalar.copy(
-                out=grouped[:]
-                .rearrange("p g b t -> p g (b t)")
-                .bitcast(F32)
-                .rearrange("p g (b u) -> p g b u", u=2),
-                in_=x_turned[:].rearrange("p (g u b) -> p g b u", g=PASSES, u=2),
+            copy_on(
+                engine,
+                grouped[:].rearrange("p g b t -> p g (b t)").bitcast(F32).rearrange("p g (b u) -> p g b u", u=2),
+                x_turned[:].rearrange("p (g u b) -> p g b u", g=PASSES, u=2),
             )
             return grouped
 
@@ -137,13 +156,12 @@ def tile_middlelayer_kernel(tc, in_data, W_words, W_scales, bias, out):
                     in_=grouped[:, g].rearrange("p b t -> p (b t)"),
                 )
 
-        def product(n_tile, run):
-            bank = products.tile([P, B_RUN], F32, name="product", tag="bank")
+        def product(acc, n_tile, b_from, b_tiles):
             n_cols = slice(n_tile * P, (n_tile + 1) * P)
-            b_cols = slice(run * B_RUN, (run + 1) * B_RUN)
+            b_cols = slice(b_from * P, (b_from + b_tiles) * P)
             for g in range(PASSES):
                 nc.tensor.matmul_mx(
-                    out=bank[:],
+                    out=acc,
                     lhsT=w_codes[:, g, n_cols].bitcast(FP8X4),
                     lhsT_scale=w_scales[4 * g : P, n_cols],
                     rhs=x_codes[:, g, b_cols].bitcast(FP8X4),
@@ -151,80 +169,123 @@ def tile_middlelayer_kernel(tc, in_data, W_words, W_scales, bias, out):
                     start=(g == 0),
                     stop=(g == PASSES - 1),
                 )
-            return bank
 
-        def multiply_and_fold(rnd):
-            run, pair = divmod(rnd, ROUNDS_PER_RUN)
-            tiles = [pair * PAIR + a for a in range(PAIR)]
-            p2 = [product(J_TILES + jt, run) for jt in tiles]
-            p1 = [product(jt, run) for jt in tiles]
+        def multiply_and_fold(b_from, b_tiles, jt):
+            width = b_tiles * P
+            per_bank = BANK // width
+            accs = {}
+            for half in (1, 0):
+                for a in range(2):
+                    if a % per_bank == 0:
+                        bank = products.tile([P, BANK], F32, name="product", tag="bank")
+                    accs[(half, a)] = bank[:, (a % per_bank) * width : (a % per_bank + 1) * width]
+                    product(accs[(half, a)], half * J_TILES + jt + a, b_from, b_tiles)
             relu2 = []
-            for a, jt in enumerate(tiles):
-                relu2.append(fold.tile([P, B_RUN], F32, name="relu2"))
-                nc.vector.tensor_scalar(
-                    out=relu2[a][:],
-                    in0=p2[a][:],
-                    scalar1=b2_minus_b1[:, jt : jt + 1],
-                    scalar2=neg_b1[:, jt : jt + 1],
-                    op0=ALU.add,
-                    op1=ALU.max,
-                )
+            for a in range(2):
+                t = fold.tile([P, width], F32, name="relu2")
+                nc.vector.tensor_scalar(out=t[:], in0=accs[(1, a)], scalar1=b2_minus_b1[:, jt + a : jt + a + 1],
+                                        scalar2=neg_b1[:, jt + a : jt + a + 1], op0=ALU.add, op1=ALU.max)
+                relu2.append(t)
             r_tiles = []
-            for a, jt in enumerate(tiles):
-                r_tiles.append(folded.tile([P, B_RUN], F32, name="r_tile"))
-                nc.vector.scalar_tensor_tensor(
-                    out=r_tiles[a][:],
-                    in0=p1[a][:],
-                    scalar=neg_b1[:, jt : jt + 1],
-                    in1=relu2[a][:],
-                    op0=ALU.max,
-                    op1=ALU.subtract,
-                )
+            for a in range(2):
+                t = folded.tile([P, width], F32, name="r_tile")
+                nc.vector.scalar_tensor_tensor(out=t[:], in0=accs[(0, a)], scalar=neg_b1[:, jt + a : jt + a + 1],
+                                               in1=relu2[a][:], op0=ALU.max, op1=ALU.subtract)
+                r_tiles.append(t)
             return r_tiles
 
-        def turn_and_store(rnd, r_tiles):
-            run, pair = divmod(rnd, ROUNDS_PER_RUN)
-            width = 2 * PAIR * P
-            for q in range(RUN_TILES):
-                bank = turned_banks[q]
-                for a in range(PAIR):
-                    nc.tensor.transpose(
-                        out=bank[:, a * P : (a + 1) * P],
-                        in_=r_tiles[a][:, q * P : (q + 1) * P],
-                        identity=identity[:],
-                    )
-                copy_out = nc.vector.tensor_copy if rnd == ROUNDS - 1 else nc.scalar.copy
+        def turn_and_store(b_from, b_tiles, jt, r_pairs, engines):
+            slot = 0
+            width = 4 * P * len(r_pairs)
+            for q in range(b_tiles):
                 rows = rows_out.tile([P, width], F32, name="rows")
-                copy_out(
-                    out=rows[:].rearrange("p (c e) -> p c e", e=2),
-                    in_=bank[:].rearrange("p (e c) -> p c e", e=2),
-                )
-                bt = run * RUN_TILES + q
-                nc.sync.dma_start(
-                    out=out_rows[bt * P : (bt + 1) * P, pair * width : (pair + 1) * width],
-                    in_=rows[:],
-                )
+                for h, r_tiles in enumerate(r_pairs):
+                    bank = turned_banks[slot]
+                    for a in range(2):
+                        nc.tensor.transpose(out=bank[:, a * P : (a + 1) * P], in_=r_tiles[a][:, q * P : (q + 1) * P], identity=identity[:])
+                    copy_on(engines[slot % len(engines)],
+                            rows[:, h * BANK : (h + 1) * BANK].rearrange("p (c e) -> p c e", e=2),
+                            bank[:].rearrange("p (e c) -> p c e", e=2))
+                    slot += 1
+                bt = b_from + q
+                nc.sync.dma_start(out=out_rows[bt * P : (bt + 1) * P, 2 * jt * P : 2 * jt * P + width], in_=rows[:])
 
-        grouped_tiles = {}
-        x_imags = {0: take_imaginary(0)}
-        for bt in range(RUN_TILES):
-            if bt + 1 < RUN_TILES:
-                x_imags[bt + 1] = take_imaginary(bt + 1)
-            grouped_tiles[bt] = transpose_x(x_imags[bt])
+        def unit_multiply(bt, c):
+            b_cols = slice(bt * P, (bt + 1) * P)
+            sums = sums_pool.tile([P, 2, BANK], F32, name="sums")
+            banks = {}
+            for s in (1, 0):
+                banks[s] = products.tile([P, BANK], F32, name="unit_bank", tag="bank")
+                n_cols = slice(s * J + JX + c * BANK, s * J + JX + (c + 1) * BANK)
+                for g in range(PASSES):
+                    nc.tensor.matmul_mx(
+                        out=banks[s][:],
+                        lhsT=x_codes[:, g, b_cols].bitcast(FP8X4),
+                        lhsT_scale=x_scales[:, g, b_cols],
+                        rhs=w_codes[:, g, n_cols].bitcast(FP8X4),
+                        rhs_scale=w_scales[4 * g : P, n_cols],
+                        start=(g == 0),
+                        stop=(g == PASSES - 1),
+                    )
+            for s in (1, 0):
+                nc.vector.tensor_tensor(out=sums[:, s, :], in0=banks[s][:], in1=bias_all[:, s, c * BANK : (c + 1) * BANK], op=ALU.add)
+            return sums
+
+        def unit_relu(sums):
+            acts = acts_pool.tile([P, 2, BANK], F32, name="acts")
+            nc.scalar.activation(out=acts[:], in_=sums[:], func=ACT.Relu)
+            return acts
+
+        used = []
+
+        def unit_fold(acts):
+            rows = wide_rows[len(used) % WIDE_ROWS]
+            used.append(0)
+            nc.gpsimd.tensor_tensor(out=rows[:].rearrange("p (c e) -> p c e", e=2)[:, :, 0], in0=acts[:, 0, :], in1=acts[:, 1, :], op=ALU.subtract)
+            return rows
+
+        def unit_store(bt, c, rows):
+            col = 2 * (JX + c * BANK)
+            nc.sync.dma_start(out=out_rows[bt * P : (bt + 1) * P, col : col + 2 * BANK], in_=rows[:])
+
+        SPLIT = ("vector", "scalar")
+        imag = {0: take_imaginary(0, SPLIT)}
+        grouped = {}
+        for bt in range(4):
+            if bt + 1 < 4:
+                imag[bt + 1] = take_imaginary(bt + 1, SPLIT)
+            grouped[bt] = transpose_x(imag[bt], "scalar")
+            if bt == 0:
+                bias_to_partitions()
             if bt >= 1:
-                quantise_x(bt - 1, grouped_tiles[bt - 1])
-        quantise_x(RUN_TILES - 1, grouped_tiles[RUN_TILES - 1])
+                quantise_x(bt - 1, grouped[bt - 1])
+        quantise_x(3, grouped[3])
 
-        r_tiles = {}
-        for rnd in range(ROUNDS + 1):
-            prepares_x = RUN_TILES <= rnd < B_TILES
+        rounds = [(b_from, 4, jt) for b_from in (0, 4) for jt in range(0, JX_TILES, 2)]
+        per_run = JX_TILES // 2
+        pending = None
+        waiting = []
+        for i, (b_from, b_tiles, jt) in enumerate(rounds):
+            prepares_x = 2 <= i < 6
             if prepares_x:
-                x_imag = take_imaginary(rnd)
-            if rnd < ROUNDS:
-                r_tiles[rnd] = multiply_and_fold(rnd)
+                imag[2 + i] = take_imaginary(2 + i, SPLIT)
+            r = multiply_and_fold(b_from, b_tiles, jt)
+            sums = []
+            if per_run <= i < per_run + 3:
+                sums = [(bt, unit_multiply(bt, 0)) for bt in range(3 * (i - per_run), min(3 * (i - per_run) + 3, B_TILES))]
+            if i < 2:
+                nc.scalar.copy(out=wide_rows[2 + i][:], in_=zeros[:])
+            if i == 1:
+                for s in (1, 0):
+                    spread_bias(s, 0, "scalar")
             if prepares_x:
-                grouped_tiles[rnd] = transpose_x(x_imag)
-            if rnd >= 1:
-                turn_and_store(rnd - 1, r_tiles[rnd - 1])
+                grouped[2 + i] = transpose_x(imag[2 + i], "scalar")
+            for w in waiting:
+                unit_store(*w)
+            if pending:
+                turn_and_store(*pending, ("scalar",))
+            waiting = [(bt, 0, unit_fold(unit_relu(sm))) for bt, sm in sums]
             if prepares_x:
-                quantise_x(rnd, grouped_tiles[rnd])
+                quantise_x(2 + i, grouped[2 + i])
+            pending = (b_from, b_tiles, jt, [r])
+        turn_and_store(*pending, ("scalar", "vector"))

@@ -24,7 +24,7 @@ BANK = 512
 JX = 1536
 JX_TILES = JX // P
 CHUNKS = (J - JX) // BANK
-WIDE_ROWS = 4
+WIDE_ROWS = 3
 
 FLOPS = 2 * B * K * N
 
@@ -40,8 +40,8 @@ def tile_middlelayer_kernel(tc, in_data, W_words, W_scales, bias, out):
         fold = ctx.enter_context(tc.tile_pool(name="fold", bufs=4))
         folded = ctx.enter_context(tc.tile_pool(name="folded", bufs=8))
         rows_out = ctx.enter_context(tc.tile_pool(name="rows_out", bufs=16))
-        sums_pool = ctx.enter_context(tc.tile_pool(name="sums_pool", bufs=3))
-        acts_pool = ctx.enter_context(tc.tile_pool(name="acts_pool", bufs=5))
+        sums_pool = ctx.enter_context(tc.tile_pool(name="sums_pool", bufs=5))
+        wide_pool = ctx.enter_context(tc.tile_pool(name="wide_pool", bufs=4))
         products = ctx.enter_context(tc.psum_pool(name="products", bufs=4))
         turned = ctx.enter_context(tc.psum_pool(name="turned", bufs=1))
 
@@ -58,7 +58,7 @@ def tile_middlelayer_kernel(tc, in_data, W_words, W_scales, bias, out):
         b2_minus_b1 = keep.tile([P, J_TILES], F32, name="b2_minus_b1")
         identity_bf16 = keep.tile([P, P], BF16, name="identity_bf16")
         bias_all = keep.tile([P, 2, J - JX], F32, name="bias_all")
-        wide_rows = [keep.tile([P, 2 * BANK], F32, name="wide_rows%d" % i) for i in range(WIDE_ROWS)]
+        wide_rows = [keep.tile([P, 2, BANK], F32, name="wide_rows%d" % i) for i in range(WIDE_ROWS)]
 
         def load_x(bt):
             nc.sync.dma_start(out=x_raw[bt][:], in_=in_data[bt * P : (bt + 1) * P, :])
@@ -80,8 +80,8 @@ def tile_middlelayer_kernel(tc, in_data, W_words, W_scales, bias, out):
         make_identity(nc, identity_bf16[:])
         nc.vector.memset(zeros[:].bitcast(I32), 0)
         nc.vector.memset(w_scales[:].bitcast(I32), 0)
-        for rows in wide_rows[0:2]:
-            nc.scalar.copy(out=rows[:], in_=zeros[:])
+        for rows in wide_rows:
+            nc.scalar.copy(out=rows[:, 1, :], in_=zeros[:, 0:BANK])
         for quadrant in range(4):
             nc.sync.dma_start(
                 out=w_scales[32 * quadrant : 32 * quadrant + 4 * PASSES, :].bitcast(I32),
@@ -90,10 +90,10 @@ def tile_middlelayer_kernel(tc, in_data, W_words, W_scales, bias, out):
         load_w(0, 2)
         load_w(2, 4)
         load_w(4, 8)
-        load_w(8, 12)
+        load_w(12, 16)
         for bt in range(4, B_TILES):
             load_x(bt)
-        load_w(12, 16)
+        load_w(8, 12)
 
         turned_banks = [turned.tile([P, BANK], F32, name="turned%d" % q) for q in range(4)]
         for q in range(4):
@@ -232,16 +232,17 @@ def tile_middlelayer_kernel(tc, in_data, W_words, W_scales, bias, out):
             return sums
 
         def unit_relu(sums):
-            acts = acts_pool.tile([P, 2, BANK], F32, name="acts")
-            nc.scalar.activation(out=acts[:], in_=sums[:], func=ACT.Relu)
-            return acts
+            nc.scalar.activation(out=sums[:, 1, :], in_=sums[:, 1, :], func=ACT.Relu)
+            return sums
 
         used = []
 
-        def unit_fold(acts):
-            rows = wide_rows[len(used) % WIDE_ROWS]
+        def unit_fold(sums):
+            pair = wide_rows[len(used) % WIDE_ROWS]
             used.append(0)
-            nc.gpsimd.tensor_tensor(out=rows[:].rearrange("p (c e) -> p c e", e=2)[:, :, 0], in0=acts[:, 0, :], in1=acts[:, 1, :], op=ALU.subtract)
+            nc.vector.scalar_tensor_tensor(out=pair[:, 0, :], in0=sums[:, 0, :], scalar=0.0, in1=sums[:, 1, :], op0=ALU.max, op1=ALU.subtract)
+            rows = wide_pool.tile([P, 2 * BANK], F32, name="wide")
+            nc.scalar.copy(out=rows[:].rearrange("p (c e) -> p c e", e=2), in_=pair[:].rearrange("p e c -> p c e"))
             return rows
 
         def unit_store(bt, c, rows):
@@ -271,11 +272,9 @@ def tile_middlelayer_kernel(tc, in_data, W_words, W_scales, bias, out):
                 imag[2 + i] = take_imaginary(2 + i, SPLIT)
             r = multiply_and_fold(b_from, b_tiles, jt)
             sums = []
-            if per_run <= i < per_run + 3:
-                sums = [(bt, unit_multiply(bt, 0)) for bt in range(3 * (i - per_run), min(3 * (i - per_run) + 3, B_TILES))]
-            if i < 2:
-                nc.scalar.copy(out=wide_rows[2 + i][:], in_=zeros[:])
-            if i == 1:
+            if 3 <= i < 11:
+                sums = [(bt, unit_relu(unit_multiply(bt, 0))) for bt in (i - 3,)]
+            if i == 0:
                 for s in (1, 0):
                     spread_bias(s, 0, "scalar")
             if prepares_x:
@@ -284,7 +283,7 @@ def tile_middlelayer_kernel(tc, in_data, W_words, W_scales, bias, out):
                 unit_store(*w)
             if pending:
                 turn_and_store(*pending, ("scalar",))
-            waiting = [(bt, 0, unit_fold(unit_relu(sm))) for bt, sm in sums]
+            waiting = [(bt, 0, unit_fold(sm)) for bt, sm in sums]
             if prepares_x:
                 quantise_x(2 + i, grouped[2 + i])
             pending = (b_from, b_tiles, jt, [r])

@@ -261,6 +261,8 @@ def tile_middlelayer_kernel(tc, in_data, W_words, W_scales, bias, out):
             if bt >= 1:
                 quantise_x(bt - 1, grouped[bt - 1])
         quantise_x(3, grouped[3])
+        for s in (1, 0):
+            spread_bias(s, 0, "scalar")
 
         rounds = [(b_from, 4, jt) for b_from in (0, 4) for jt in range(0, JX_TILES, 2)]
         per_run = JX_TILES // 2
@@ -272,11 +274,9 @@ def tile_middlelayer_kernel(tc, in_data, W_words, W_scales, bias, out):
                 imag[2 + i] = take_imaginary(2 + i, SPLIT)
             r = multiply_and_fold(b_from, b_tiles, jt)
             sums = []
+            sums = []
             if 3 <= i < 11:
                 sums = [(bt, unit_relu(unit_multiply(bt, 0))) for bt in (i - 3,)]
-            if i == 0:
-                for s in (1, 0):
-                    spread_bias(s, 0, "scalar")
             if prepares_x:
                 grouped[2 + i] = transpose_x(imag[2 + i], "scalar")
             for w in waiting:

@@ -274,15 +274,14 @@ def tile_middlelayer_kernel(tc, in_data, W_words, W_scales, bias, out):
                 imag[2 + i] = take_imaginary(2 + i, SPLIT)
             r = multiply_and_fold(b_from, b_tiles, jt)
             sums = []
-            sums = []
-            if 3 <= i < 11:
-                sums = [(bt, unit_relu(unit_multiply(bt, 0))) for bt in (i - 3,)]
+            if 2 <= i < 10:
+                sums = [(bt, unit_relu(unit_multiply(bt, 0))) for bt in (i - 2,)]
             if prepares_x:
                 grouped[2 + i] = transpose_x(imag[2 + i], "scalar")
             for w in waiting:
                 unit_store(*w)
             if pending:
-                turn_and_store(*pending, ("scalar",))
+                turn_and_store(*pending, ("scalar",) if i < len(rounds) - 1 else ("scalar", "vector"))
             waiting = [(bt, 0, unit_fold(sm)) for bt, sm in sums]
             if prepares_x:
                 quantise_x(2 + i, grouped[2 + i])

@@ -89,10 +89,12 @@ def tile_middlelayer_kernel(tc, in_data, W_words, W_scales, bias, out):
             )
         load_w(0, 2)
         load_w(2, 4)
+        load_x(4)
         load_w(4, 8)
+        load_x(5)
         load_w(12, 16)
-        for bt in range(4, B_TILES):
-            load_x(bt)
+        load_x(6)
+        load_x(7)
         load_w(8, 12)
 
         turned_banks = [turned.tile([P, BANK], F32, name="turned%d" % q) for q in range(4)]
@@ -269,21 +271,21 @@ def tile_middlelayer_kernel(tc, in_data, W_words, W_scales, bias, out):
         pending = None
         waiting = []
         for i, (b_from, b_tiles, jt) in enumerate(rounds):
-            prepares_x = 2 <= i < 6
+            prepares_x = 1 <= i < 5
             if prepares_x:
-                imag[2 + i] = take_imaginary(2 + i, SPLIT)
+                imag[3 + i] = take_imaginary(3 + i, SPLIT)
             r = multiply_and_fold(b_from, b_tiles, jt)
             sums = []
             if 2 <= i < 10:
                 sums = [(bt, unit_relu(unit_multiply(bt, 0))) for bt in (i - 2,)]
             if prepares_x:
-                grouped[2 + i] = transpose_x(imag[2 + i], "scalar")
+                grouped[3 + i] = transpose_x(imag[3 + i], "scalar")
             for w in waiting:
                 unit_store(*w)
             if pending:
                 turn_and_store(*pending, ("scalar",) if i < len(rounds) - 1 else ("scalar", "vector"))
             waiting = [(bt, 0, unit_fold(sm)) for bt, sm in sums]
             if prepares_x:
-                quantise_x(2 + i, grouped[2 + i])
+                quantise_x(3 + i, grouped[3 + i])
             pending = (b_from, b_tiles, jt, [r])
         turn_and_store(*pending, ("scalar", "vector"))

@@ -23,8 +23,22 @@ J_TILES = J // P
 BANK = 512
 JX = 1536
 JX_TILES = JX // P
-CHUNKS = (J - JX) // BANK
 WIDE_ROWS = 3
+PRODUCT_BANKS = 4
+
+RUNS = ((0, 4), (4, 4))
+HEAD_TILES = 4
+X_AT = {1: 4, 2: 5, 3: 6, 4: 7}
+UNITS_AT = {2: (0,), 3: (1,), 4: (2,), 5: (3,), 6: (4,), 7: (5,), 8: (6,), 9: (7,)}
+BIAS_AT = -1
+FOLD_BUFS = 4
+FOLDED_BUFS = 8
+ROWS_BUFS = 16
+STORE_GROUPS = ((1, 1, 1, 1, 1, 1), (1, 1, 1, 1, 1, 1))
+LOADS = (("x", 0), ("x", 1), ("x", 2), ("x", 3), ("s",), ("w", 0, 2), ("w", 2, 4), ("x", 4), ("w", 4, 8), ("x", 5), ("w", 12, 16), ("x", 6), ("x", 7), ("w", 8, 12))
+SHARE_FROM = 11
+SHARE = ("scalar", "vector")
+ROUNDS = ((0, 4, 0, 2), (0, 4, 2, 2), (0, 4, 4, 2), (0, 4, 6, 2), (0, 4, 8, 2), (0, 4, 10, 2), (4, 4, 0, 2), (4, 4, 2, 2), (4, 4, 4, 2), (4, 4, 6, 2), (4, 4, 8, 2), (4, 4, 10, 2))
 
 FLOPS = 2 * B * K * N
 
@@ -37,12 +51,12 @@ def tile_middlelayer_kernel(tc, in_data, W_words, W_scales, bias, out):
         ctx.enter_context(tc.manual_schedule())
         keep = ctx.enter_context(tc.tile_pool(name="keep", bufs=1))
         x_stage = ctx.enter_context(tc.tile_pool(name="x_stage", bufs=3))
-        fold = ctx.enter_context(tc.tile_pool(name="fold", bufs=4))
-        folded = ctx.enter_context(tc.tile_pool(name="folded", bufs=8))
-        rows_out = ctx.enter_context(tc.tile_pool(name="rows_out", bufs=16))
+        fold = ctx.enter_context(tc.tile_pool(name="fold", bufs=FOLD_BUFS))
+        folded = ctx.enter_context(tc.tile_pool(name="folded", bufs=FOLDED_BUFS))
+        rows_out = ctx.enter_context(tc.tile_pool(name="rows_out", bufs=ROWS_BUFS))
         sums_pool = ctx.enter_context(tc.tile_pool(name="sums_pool", bufs=5))
         wide_pool = ctx.enter_context(tc.tile_pool(name="wide_pool", bufs=4))
-        products = ctx.enter_context(tc.psum_pool(name="products", bufs=4))
+        products = ctx.enter_context(tc.psum_pool(name="products", bufs=PRODUCT_BANKS))
         turned = ctx.enter_context(tc.psum_pool(name="turned", bufs=1))
 
         x_raw = [keep.tile([P, 2 * K], BF16, name="x_raw%d" % bt) for bt in range(B_TILES)]
@@ -72,30 +86,28 @@ def tile_middlelayer_kernel(tc, in_data, W_words, W_scales, bias, out):
                     in_=words.rearrange("p (s n) -> p s n", s=2)[:, :, cols],
                 )
 
+        def load_scales():
+            for quadrant in range(4):
+                nc.sync.dma_start(
+                    out=w_scales[32 * quadrant : 32 * quadrant + 4 * PASSES, :].bitcast(I32),
+                    in_=W_scales[:, 4 * quadrant : 4 * quadrant + 4, :].bitcast(I32),
+                )
+
         nc.vector.memset(bias_rows[:], 0.0)
         nc.scalar.dma_start(out=bias_rows[0 : N // P, :], in_=bias.rearrange("(r c) -> r c", c=P))
-        for bt in range(4):
-            load_x(bt)
-        make_identity(nc, identity[:])
-        make_identity(nc, identity_bf16[:])
-        nc.vector.memset(zeros[:].bitcast(I32), 0)
-        nc.vector.memset(w_scales[:].bitcast(I32), 0)
-        for rows in wide_rows:
-            nc.scalar.copy(out=rows[:, 1, :], in_=zeros[:, 0:BANK])
-        for quadrant in range(4):
-            nc.sync.dma_start(
-                out=w_scales[32 * quadrant : 32 * quadrant + 4 * PASSES, :].bitcast(I32),
-                in_=W_scales[:, 4 * quadrant : 4 * quadrant + 4, :].bitcast(I32),
-            )
-        load_w(0, 2)
-        load_w(2, 4)
-        load_x(4)
-        load_w(4, 8)
-        load_x(5)
-        load_w(12, 16)
-        load_x(6)
-        load_x(7)
-        load_w(8, 12)
+        for what in LOADS:
+            if what[0] == "x":
+                load_x(what[1])
+            elif what[0] == "w":
+                load_w(what[1], what[2])
+            else:
+                make_identity(nc, identity[:])
+                make_identity(nc, identity_bf16[:])
+                nc.vector.memset(zeros[:].bitcast(I32), 0)
+                nc.vector.memset(w_scales[:].bitcast(I32), 0)
+                for rows in wide_rows:
+                    nc.scalar.copy(out=rows[:, 1, :], in_=zeros[:, 0:BANK])
+                load_scales()
 
         turned_banks = [turned.tile([P, BANK], F32, name="turned%d" % q) for q in range(4)]
         for q in range(4):
@@ -172,45 +184,52 @@ def tile_middlelayer_kernel(tc, in_data, W_words, W_scales, bias, out):
                     stop=(g == PASSES - 1),
                 )
 
-        def multiply_and_fold(b_from, b_tiles, jt):
+        def multiply_and_fold(b_from, b_tiles, jt, n_j, between):
             width = b_tiles * P
             per_bank = BANK // width
             accs = {}
             for half in (1, 0):
-                for a in range(2):
+                for a in range(n_j):
                     if a % per_bank == 0:
                         bank = products.tile([P, BANK], F32, name="product", tag="bank")
                     accs[(half, a)] = bank[:, (a % per_bank) * width : (a % per_bank + 1) * width]
                     product(accs[(half, a)], half * J_TILES + jt + a, b_from, b_tiles)
             relu2 = []
-            for a in range(2):
+            for a in range(n_j):
                 t = fold.tile([P, width], F32, name="relu2")
                 nc.vector.tensor_scalar(out=t[:], in0=accs[(1, a)], scalar1=b2_minus_b1[:, jt + a : jt + a + 1],
                                         scalar2=neg_b1[:, jt + a : jt + a + 1], op0=ALU.add, op1=ALU.max)
                 relu2.append(t)
+            between()
             r_tiles = []
-            for a in range(2):
+            for a in range(n_j):
                 t = folded.tile([P, width], F32, name="r_tile")
                 nc.vector.scalar_tensor_tensor(out=t[:], in0=accs[(0, a)], scalar=neg_b1[:, jt + a : jt + a + 1],
                                                in1=relu2[a][:], op0=ALU.max, op1=ALU.subtract)
                 r_tiles.append(t)
             return r_tiles
 
-        def turn_and_store(b_from, b_tiles, jt, r_pairs, engines):
+        shared_rows = {}
+
+        def turn_and_store(b_from, b_tiles, jt, n_j, r_tiles, part, parts, engines):
             slot = 0
-            width = 4 * P * len(r_pairs)
+            width = 2 * P * n_j
             for q in range(b_tiles):
-                rows = rows_out.tile([P, width], F32, name="rows")
-                for h, r_tiles in enumerate(r_pairs):
+                if part == 0:
+                    shared_rows[q] = rows_out.tile([P, width * parts], F32, name="rows")
+                rows = shared_rows[q]
+                for h in range(n_j // 2):
                     bank = turned_banks[slot]
                     for a in range(2):
-                        nc.tensor.transpose(out=bank[:, a * P : (a + 1) * P], in_=r_tiles[a][:, q * P : (q + 1) * P], identity=identity[:])
+                        nc.tensor.transpose(out=bank[:, a * P : (a + 1) * P], in_=r_tiles[2 * h + a][:, q * P : (q + 1) * P], identity=identity[:])
                     copy_on(engines[slot % len(engines)],
-                            rows[:, h * BANK : (h + 1) * BANK].rearrange("p (c e) -> p c e", e=2),
+                            rows[:, part * width + h * BANK : part * width + (h + 1) * BANK].rearrange("p (c e) -> p c e", e=2),
                             bank[:].rearrange("p (e c) -> p c e", e=2))
                     slot += 1
                 bt = b_from + q
-                nc.sync.dma_start(out=out_rows[bt * P : (bt + 1) * P, 2 * jt * P : 2 * jt * P + width], in_=rows[:])
+                if part == parts - 1:
+                    col = 2 * (jt + n_j) * P
+                    nc.sync.dma_start(out=out_rows[bt * P : (bt + 1) * P, col - width * parts : col], in_=rows[:])
 
         def unit_multiply(bt, c):
             b_cols = slice(bt * P, (bt + 1) * P)
@@ -239,53 +258,52 @@ def tile_middlelayer_kernel(tc, in_data, W_words, W_scales, bias, out):
 
         used = []
 
-        def unit_fold(sums):
+        def unit_finish(bt, c, sums):
             pair = wide_rows[len(used) % WIDE_ROWS]
             used.append(0)
             nc.vector.scalar_tensor_tensor(out=pair[:, 0, :], in0=sums[:, 0, :], scalar=0.0, in1=sums[:, 1, :], op0=ALU.max, op1=ALU.subtract)
             rows = wide_pool.tile([P, 2 * BANK], F32, name="wide")
             nc.scalar.copy(out=rows[:].rearrange("p (c e) -> p c e", e=2), in_=pair[:].rearrange("p e c -> p c e"))
-            return rows
-
-        def unit_store(bt, c, rows):
             col = 2 * (JX + c * BANK)
             nc.sync.dma_start(out=out_rows[bt * P : (bt + 1) * P, col : col + 2 * BANK], in_=rows[:])
 
         SPLIT = ("vector", "scalar")
         imag = {0: take_imaginary(0, SPLIT)}
         grouped = {}
-        for bt in range(4):
-            if bt + 1 < 4:
+        for bt in range(HEAD_TILES):
+            if bt + 1 < HEAD_TILES:
                 imag[bt + 1] = take_imaginary(bt + 1, SPLIT)
             grouped[bt] = transpose_x(imag[bt], "scalar")
             if bt == 0:
                 bias_to_partitions()
             if bt >= 1:
                 quantise_x(bt - 1, grouped[bt - 1])
-        quantise_x(3, grouped[3])
-        for s in (1, 0):
-            spread_bias(s, 0, "scalar")
+        quantise_x(HEAD_TILES - 1, grouped[HEAD_TILES - 1])
+        if BIAS_AT < 0:
+            for s in (1, 0):
+                spread_bias(s, 0, "scalar")
 
-        rounds = [(b_from, 4, jt) for b_from in (0, 4) for jt in range(0, JX_TILES, 2)]
-        per_run = JX_TILES // 2
+        rounds = [rd + (0, 1) for rd in ROUNDS]
         pending = None
-        waiting = []
-        for i, (b_from, b_tiles, jt) in enumerate(rounds):
-            prepares_x = 1 <= i < 5
-            if prepares_x:
-                imag[3 + i] = take_imaginary(3 + i, SPLIT)
-            r = multiply_and_fold(b_from, b_tiles, jt)
-            sums = []
-            if 2 <= i < 10:
-                sums = [(bt, unit_relu(unit_multiply(bt, 0))) for bt in (i - 2,)]
-            if prepares_x:
-                grouped[3 + i] = transpose_x(imag[3 + i], "scalar")
-            for w in waiting:
-                unit_store(*w)
+        open_units = []
+
+        def finish_units():
+            for u in open_units:
+                unit_finish(*u)
+            open_units.clear()
+
+        for i, (b_from, b_tiles, jt, n_j, part, parts) in enumerate(rounds):
+            tile_x = X_AT.get(i)
+            if tile_x is not None:
+                imag[tile_x] = take_imaginary(tile_x, SPLIT)
+            r = multiply_and_fold(b_from, b_tiles, jt, n_j, finish_units)
+            open_units.extend([(bt, 0, unit_relu(unit_multiply(bt, 0))) for bt in UNITS_AT.get(i, ())])
+            if tile_x is not None:
+                grouped[tile_x] = transpose_x(imag[tile_x], "scalar")
             if pending:
-                turn_and_store(*pending, ("scalar",) if i < len(rounds) - 1 else ("scalar", "vector"))
-            waiting = [(bt, 0, unit_fold(sm)) for bt, sm in sums]
-            if prepares_x:
-                quantise_x(3 + i, grouped[3 + i])
-            pending = (b_from, b_tiles, jt, [r])
-        turn_and_store(*pending, ("scalar", "vector"))
+                turn_and_store(*pending, ("scalar",) if i < SHARE_FROM else SHARE)
+            if tile_x is not None:
+                quantise_x(tile_x, grouped[tile_x])
+            pending = (b_from, b_tiles, jt, n_j, r, part, parts)
+        finish_units()
+        turn_and_store(*pending, SHARE)

@@ -35,7 +35,7 @@ FOLD_BUFS = 4
 FOLDED_BUFS = 8
 ROWS_BUFS = 16
 STORE_GROUPS = ((1, 1, 1, 1, 1, 1), (1, 1, 1, 1, 1, 1))
-LOADS = (("x", 0), ("x", 1), ("x", 2), ("x", 3), ("s",), ("w", 0, 2), ("w", 2, 4), ("x", 4), ("w", 4, 8), ("x", 5), ("w", 12, 16), ("x", 6), ("x", 7), ("w", 8, 12))
+LOADS = (("x", 0), ("x", 1), ("x", 2), ("x", 3), ("s",), ("w", 0, 2), ("w", 2, 4), ("x", 4), ("w", 4, 6), ("x", 5), ("w", 12, 16), ("w", 6, 8), ("x", 6), ("x", 7), ("w", 8, 12))
 SHARE_FROM = 11
 SHARE = ("scalar", "vector")
 ROUNDS = ((0, 4, 0, 2), (0, 4, 2, 2), (0, 4, 4, 2), (0, 4, 6, 2), (0, 4, 8, 2), (0, 4, 10, 2), (4, 4, 0, 2), (4, 4, 2, 2), (4, 4, 4, 2), (4, 4, 6, 2), (4, 4, 8, 2), (4, 4, 10, 2))

@@ -29,7 +29,7 @@ PRODUCT_BANKS = 4
 RUNS = ((0, 4), (4, 4))
 HEAD_TILES = 4
 X_AT = {1: 4, 2: 5, 3: 6, 4: 7}
-UNITS_AT = {2: (0,), 3: (1,), 4: (2,), 5: (3,), 6: (4,), 7: (5,), 8: (6,), 9: (7,)}
+UNITS_AT = {2: ((0, 0),), 3: ((1, 0),), 4: ((2, 0),), 5: ((3, 0),), 6: ((4, 0),), 7: ((5, 0),), 8: ((6, 0),), 9: ((7, 0),)}
 BIAS_AT = -1
 FOLD_BUFS = 4
 FOLDED_BUFS = 8
@@ -39,6 +39,9 @@ LOADS = (("x", 0), ("x", 1), ("x", 2), ("x", 3), ("s",), ("w", 0, 2), ("w", 2, 4
 SHARE_FROM = 11
 SHARE = ("scalar", "vector")
 ROUNDS = ((0, 4, 0, 2), (0, 4, 2, 2), (0, 4, 4, 2), (0, 4, 6, 2), (0, 4, 8, 2), (0, 4, 10, 2), (4, 4, 0, 2), (4, 4, 2, 2), (4, 4, 4, 2), (4, 4, 6, 2), (4, 4, 8, 2), (4, 4, 10, 2))
+UB = 1536
+SUMS_BUFS = 5
+WIDE_BUFS = 4
 
 FLOPS = 2 * B * K * N
 
@@ -54,8 +57,8 @@ def tile_middlelayer_kernel(tc, in_data, W_words, W_scales, bias, out):
         fold = ctx.enter_context(tc.tile_pool(name="fold", bufs=FOLD_BUFS))
         folded = ctx.enter_context(tc.tile_pool(name="folded", bufs=FOLDED_BUFS))
         rows_out = ctx.enter_context(tc.tile_pool(name="rows_out", bufs=ROWS_BUFS))
-        sums_pool = ctx.enter_context(tc.tile_pool(name="sums_pool", bufs=5))
-        wide_pool = ctx.enter_context(tc.tile_pool(name="wide_pool", bufs=4))
+        sums_pool = ctx.enter_context(tc.tile_pool(name="sums_pool", bufs=SUMS_BUFS))
+        wide_pool = ctx.enter_context(tc.tile_pool(name="wide_pool", bufs=WIDE_BUFS))
         products = ctx.enter_context(tc.psum_pool(name="products", bufs=PRODUCT_BANKS))
         turned = ctx.enter_context(tc.psum_pool(name="turned", bufs=1))
 
@@ -71,7 +74,7 @@ def tile_middlelayer_kernel(tc, in_data, W_words, W_scales, bias, out):
         neg_b1 = keep.tile([P, J_TILES], F32, name="neg_b1")
         b2_minus_b1 = keep.tile([P, J_TILES], F32, name="b2_minus_b1")
         identity_bf16 = keep.tile([P, P], BF16, name="identity_bf16")
-        bias_all = keep.tile([P, 2, J - JX], F32, name="bias_all")
+        bias_all = keep.tile([P, 2, J - UB], F32, name="bias_all")
         wide_rows = [keep.tile([P, 2, BANK], F32, name="wide_rows%d" % i) for i in range(WIDE_ROWS)]
 
         def load_x(bt):
@@ -130,7 +133,7 @@ def tile_middlelayer_kernel(tc, in_data, W_words, W_scales, bias, out):
             bank = products.tile([P, BANK], F32, name="bias_bank", tag="bank")
             cols = slice(c * BANK, (c + 1) * BANK)
             for i in range(BANK // P):
-                row = (s * J + JX + c * BANK) // P + i
+                row = (s * J + UB + c * BANK) // P + i
                 nc.tensor.matmul(
                     out=bank[:, i * P : (i + 1) * P],
                     lhsT=identity_bf16[:, row : row + 1].to_broadcast([P, P]),
@@ -237,7 +240,7 @@ def tile_middlelayer_kernel(tc, in_data, W_words, W_scales, bias, out):
             banks = {}
             for s in (1, 0):
                 banks[s] = products.tile([P, BANK], F32, name="unit_bank", tag="bank")
-                n_cols = slice(s * J + JX + c * BANK, s * J + JX + (c + 1) * BANK)
+                n_cols = slice(s * J + UB + c * BANK, s * J + UB + (c + 1) * BANK)
                 for g in range(PASSES):
                     nc.tensor.matmul_mx(
                         out=banks[s][:],
@@ -253,7 +256,7 @@ def tile_middlelayer_kernel(tc, in_data, W_words, W_scales, bias, out):
             return sums
 
         def unit_relu(sums):
-            nc.scalar.activation(out=sums[:, 1, :], in_=sums[:, 1, :], func=ACT.Relu)
+            nc.scalar.activation(out=sums[:], in_=sums[:], func=ACT.Relu)
             return sums
 
         used = []
@@ -261,10 +264,10 @@ def tile_middlelayer_kernel(tc, in_data, W_words, W_scales, bias, out):
         def unit_finish(bt, c, sums):
             pair = wide_rows[len(used) % WIDE_ROWS]
             used.append(0)
-            nc.vector.scalar_tensor_tensor(out=pair[:, 0, :], in0=sums[:, 0, :], scalar=0.0, in1=sums[:, 1, :], op0=ALU.max, op1=ALU.subtract)
+            nc.gpsimd.tensor_tensor(out=pair[:, 0, :], in0=sums[:, 0, :], in1=sums[:, 1, :], op=ALU.subtract)
             rows = wide_pool.tile([P, 2 * BANK], F32, name="wide")
-            nc.scalar.copy(out=rows[:].rearrange("p (c e) -> p c e", e=2), in_=pair[:].rearrange("p e c -> p c e"))
-            col = 2 * (JX + c * BANK)
+            nc.gpsimd.tensor_scalar(out=rows[:].rearrange("p (c e) -> p c e", e=2), in0=pair[:].rearrange("p e c -> p c e"), scalar1=1.0, scalar2=0.0, op0=ALU.mult, op1=ALU.add)
+            col = 2 * (UB + c * BANK)
             nc.sync.dma_start(out=out_rows[bt * P : (bt + 1) * P, col : col + 2 * BANK], in_=rows[:])
 
         SPLIT = ("vector", "scalar")
@@ -279,13 +282,16 @@ def tile_middlelayer_kernel(tc, in_data, W_words, W_scales, bias, out):
             if bt >= 1:
                 quantise_x(bt - 1, grouped[bt - 1])
         quantise_x(HEAD_TILES - 1, grouped[HEAD_TILES - 1])
-        if BIAS_AT < 0:
+        for c in range((J - UB) // BANK):
             for s in (1, 0):
-                spread_bias(s, 0, "scalar")
+                spread_bias(s, c, "scalar")
 
         rounds = [rd + (0, 1) for rd in ROUNDS]
         pending = None
         open_units = []
+
+        def nothing():
+            return None
 
         def finish_units():
             for u in open_units:
@@ -296,12 +302,16 @@ def tile_middlelayer_kernel(tc, in_data, W_words, W_scales, bias, out):
             tile_x = X_AT.get(i)
             if tile_x is not None:
                 imag[tile_x] = take_imaginary(tile_x, SPLIT)
-            r = multiply_and_fold(b_from, b_tiles, jt, n_j, finish_units)
-            open_units.extend([(bt, 0, unit_relu(unit_multiply(bt, 0))) for bt in UNITS_AT.get(i, ())])
+            r = multiply_and_fold(b_from, b_tiles, jt, n_j, nothing)
+            new_units = [(bt, c, unit_multiply(bt, c)) for bt, c in UNITS_AT.get(i, ())]
             if tile_x is not None:
                 grouped[tile_x] = transpose_x(imag[tile_x], "scalar")
             if pending:
                 turn_and_store(*pending, ("scalar",) if i < SHARE_FROM else SHARE)
+            finish_units()
+            for u in new_units:
+                unit_relu(u[2])
+            open_units.extend(new_units)
             if tile_x is not None:
                 quantise_x(tile_x, grouped[tile_x])
             pending = (b_from, b_tiles, jt, n_j, r, part, parts)

@@ -29,7 +29,7 @@ PRODUCT_BANKS = 4
 RUNS = ((0, 4), (4, 4))
 HEAD_TILES = 4
 X_AT = {1: 4, 2: 5, 3: 6, 4: 7}
-UNITS_AT = {2: ((0, 0),), 3: ((1, 0),), 4: ((2, 0),), 5: ((3, 0),), 6: ((4, 0),), 7: ((5, 0),), 8: ((6, 0),), 9: ((7, 0),)}
+UNITS_AT = {2: ((0, 0, "g"),), 3: ((1, 0, "g"),), 4: ((2, 0, "g"),), 5: ((3, 0, "g"),), 6: ((4, 0, "g"),), 7: ((5, 0, "g"),), 8: ((6, 0, "g"),), 9: ((7, 0, "g"),)}
 BIAS_AT = -1
 FOLD_BUFS = 4
 FOLDED_BUFS = 8
@@ -187,27 +187,29 @@ def tile_middlelayer_kernel(tc, in_data, W_words, W_scales, bias, out):
                     stop=(g == PASSES - 1),
                 )
 
-        def multiply_and_fold(b_from, b_tiles, jt, n_j, between):
+        def multiply_half(half, b_from, b_tiles, jt, n_j):
             width = b_tiles * P
-            per_bank = BANK // width
-            accs = {}
-            for half in (1, 0):
-                for a in range(n_j):
-                    if a % per_bank == 0:
-                        bank = products.tile([P, BANK], F32, name="product", tag="bank")
-                    accs[(half, a)] = bank[:, (a % per_bank) * width : (a % per_bank + 1) * width]
-                    product(accs[(half, a)], half * J_TILES + jt + a, b_from, b_tiles)
-            relu2 = []
+            accs = []
             for a in range(n_j):
-                t = fold.tile([P, width], F32, name="relu2")
-                nc.vector.tensor_scalar(out=t[:], in0=accs[(1, a)], scalar1=b2_minus_b1[:, jt + a : jt + a + 1],
+                bank = products.tile([P, BANK], F32, name="product", tag="bank")
+                accs.append(bank[:, 0:width])
+                product(accs[a], half * J_TILES + jt + a, b_from, b_tiles)
+            return accs
+
+        def fold_first(accs, b_tiles, jt):
+            relu2 = []
+            for a, acc in enumerate(accs):
+                t = fold.tile([P, b_tiles * P], F32, name="relu2")
+                nc.vector.tensor_scalar(out=t[:], in0=acc, scalar1=b2_minus_b1[:, jt + a : jt + a + 1],
                                         scalar2=neg_b1[:, jt + a : jt + a + 1], op0=ALU.add, op1=ALU.max)
                 relu2.append(t)
-            between()
+            return relu2
+
+        def fold_second(accs, relu2, b_tiles, jt):
             r_tiles = []
-            for a in range(n_j):
-                t = folded.tile([P, width], F32, name="r_tile")
-                nc.vector.scalar_tensor_tensor(out=t[:], in0=accs[(0, a)], scalar=neg_b1[:, jt + a : jt + a + 1],
+            for a, acc in enumerate(accs):
+                t = folded.tile([P, b_tiles * P], F32, name="r_tile")
+                nc.vector.scalar_tensor_tensor(out=t[:], in0=acc, scalar=neg_b1[:, jt + a : jt + a + 1],
                                                in1=relu2[a][:], op0=ALU.max, op1=ALU.subtract)
                 r_tiles.append(t)
             return r_tiles
@@ -255,18 +257,26 @@ def tile_middlelayer_kernel(tc, in_data, W_words, W_scales, bias, out):
                 nc.vector.tensor_tensor(out=sums[:, s, :], in0=banks[s][:], in1=bias_all[:, s, c * BANK : (c + 1) * BANK], op=ALU.add)
             return sums
 
-        def unit_relu(sums):
-            nc.scalar.activation(out=sums[:], in_=sums[:], func=ACT.Relu)
-            return sums
+        def unit_relu(sums, kind):
+            if kind == "g":
+                nc.scalar.activation(out=sums[:], in_=sums[:], func=ACT.Relu)
+            else:
+                nc.scalar.activation(out=sums[:, 1, :], in_=sums[:, 1, :], func=ACT.Relu)
 
         used = []
 
-        def unit_finish(bt, c, sums):
+        def unit_finish(bt, c, sums, kind):
             pair = wide_rows[len(used) % WIDE_ROWS]
             used.append(0)
-            nc.gpsimd.tensor_tensor(out=pair[:, 0, :], in0=sums[:, 0, :], in1=sums[:, 1, :], op=ALU.subtract)
+            if kind == "g":
+                nc.gpsimd.tensor_tensor(out=pair[:, 0, :], in0=sums[:, 0, :], in1=sums[:, 1, :], op=ALU.subtract)
+            else:
+                nc.vector.scalar_tensor_tensor(out=pair[:, 0, :], in0=sums[:, 0, :], scalar=0.0, in1=sums[:, 1, :], op0=ALU.max, op1=ALU.subtract)
             rows = wide_pool.tile([P, 2 * BANK], F32, name="wide")
-            nc.gpsimd.tensor_scalar(out=rows[:].rearrange("p (c e) -> p c e", e=2), in0=pair[:].rearrange("p e c -> p c e"), scalar1=1.0, scalar2=0.0, op0=ALU.mult, op1=ALU.add)
+            if kind == "v":
+                nc.scalar.copy(out=rows[:].rearrange("p (c e) -> p c e", e=2), in_=pair[:].rearrange("p e c -> p c e"))
+            else:
+                nc.gpsimd.tensor_scalar(out=rows[:].rearrange("p (c e) -> p c e", e=2), in0=pair[:].rearrange("p e c -> p c e"), scalar1=1.0, scalar2=0.0, op0=ALU.mult, op1=ALU.add)
             col = 2 * (UB + c * BANK)
             nc.sync.dma_start(out=out_rows[bt * P : (bt + 1) * P, col : col + 2 * BANK], in_=rows[:])
 
@@ -293,27 +303,38 @@ def tile_middlelayer_kernel(tc, in_data, W_words, W_scales, bias, out):
         def nothing():
             return None
 
+        def finish_early():
+            for u in [u for u in open_units if u[3] != "g"]:
+                unit_finish(*u)
+                open_units.remove(u)
+
         def finish_units():
             for u in open_units:
                 unit_finish(*u)
             open_units.clear()
 
+        fresh_units = []
         for i, (b_from, b_tiles, jt, n_j, part, parts) in enumerate(rounds):
             tile_x = X_AT.get(i)
-            if tile_x is not None:
-                imag[tile_x] = take_imaginary(tile_x, SPLIT)
-            r = multiply_and_fold(b_from, b_tiles, jt, n_j, nothing)
-            new_units = [(bt, c, unit_multiply(bt, c)) for bt, c in UNITS_AT.get(i, ())]
+            relu2 = fold_first(multiply_half(1, b_from, b_tiles, jt, n_j), b_tiles, jt)
+            if X_AT.get(i + 1) is not None:
+                imag[X_AT[i + 1]] = take_imaginary(X_AT[i + 1], SPLIT)
             if tile_x is not None:
                 grouped[tile_x] = transpose_x(imag[tile_x], "scalar")
             if pending:
                 turn_and_store(*pending, ("scalar",) if i < SHARE_FROM else SHARE)
             finish_units()
-            for u in new_units:
-                unit_relu(u[2])
-            open_units.extend(new_units)
+            for u in fresh_units:
+                unit_relu(u[2], u[3])
+            open_units.extend(fresh_units)
+            fresh_units.clear()
+            r = fold_second(multiply_half(0, b_from, b_tiles, jt, n_j), relu2, b_tiles, jt)
+            fresh_units.extend([(bt, c, unit_multiply(bt, c), kind) for bt, c, kind in UNITS_AT.get(i, ())])
             if tile_x is not None:
                 quantise_x(tile_x, grouped[tile_x])
             pending = (b_from, b_tiles, jt, n_j, r, part, parts)
-        finish_units()
         turn_and_store(*pending, SHARE)
+        finish_units()
+        for u in fresh_units:
+            unit_relu(u[2], u[3])
+            unit_finish(*u)

@@ -28,20 +28,28 @@ PRODUCT_BANKS = 4
 
 RUNS = ((0, 4), (4, 4))
 HEAD_TILES = 4
-X_AT = {1: 4, 2: 5, 3: 6, 4: 7}
+X_AT = {2: 4, 3: 5, 4: 6, 5: 7}
 UNITS_AT = {2: ((0, 0, "g"),), 3: ((1, 0, "g"),), 4: ((2, 0, "g"),), 5: ((3, 0, "g"),), 6: ((4, 0, "g"),), 7: ((5, 0, "g"),), 8: ((6, 0, "g"),), 9: ((7, 0, "g"),)}
 BIAS_AT = -1
 FOLD_BUFS = 4
 FOLDED_BUFS = 8
 ROWS_BUFS = 16
 STORE_GROUPS = ((1, 1, 1, 1, 1, 1), (1, 1, 1, 1, 1, 1))
-LOADS = (("x", 0), ("x", 1), ("x", 2), ("x", 3), ("s",), ("w", 0, 2), ("w", 2, 4), ("x", 4), ("w", 4, 6), ("x", 5), ("w", 12, 16), ("w", 6, 8), ("x", 6), ("x", 7), ("w", 8, 12))
+LOADS = (("x", 0), ("b",), ("x", 1), ("x", 2), ("x", 3), ("s",), ("w", 0, 2), ("w", 2, 4), ("x", 4), ("w", 4, 6), ("x", 5), ("w", 12, 16), ("w", 6, 8), ("x", 6), ("x", 7), ("w", 8, 12))
 SHARE_FROM = 11
 SHARE = ("scalar", "vector")
 ROUNDS = ((0, 4, 0, 2), (0, 4, 2, 2), (0, 4, 4, 2), (0, 4, 6, 2), (0, 4, 8, 2), (0, 4, 10, 2), (4, 4, 0, 2), (4, 4, 2, 2), (4, 4, 4, 2), (4, 4, 6, 2), (4, 4, 8, 2), (4, 4, 10, 2))
 UB = 1536
 SUMS_BUFS = 5
 WIDE_BUFS = 4
+HEAD_BIAS = (0,)
+LATE_BIAS = {}
+LATE_BIAS_ENGINES = ("vector", "scalar")
+BUFFER_N = 32
+HEAD_SPLIT = ("vector", "scalar")
+ROUND_SPLIT = ("vector", "scalar")
+IMAG_EARLY = True
+QUANT_EARLY = True
 
 FLOPS = 2 * B * K * N
 
@@ -97,12 +105,13 @@ def tile_middlelayer_kernel(tc, in_data, W_words, W_scales, bias, out):
                 )
 
         nc.vector.memset(bias_rows[:], 0.0)
-        nc.scalar.dma_start(out=bias_rows[0 : N // P, :], in_=bias.rearrange("(r c) -> r c", c=P))
         for what in LOADS:
             if what[0] == "x":
                 load_x(what[1])
             elif what[0] == "w":
                 load_w(what[1], what[2])
+            elif what[0] == "b":
+                nc.sync.dma_start(out=bias_rows[0 : N // P, :], in_=bias.rearrange("(r c) -> r c", c=P))
             else:
                 make_identity(nc, identity[:])
                 make_identity(nc, identity_bf16[:])
@@ -116,6 +125,9 @@ def tile_middlelayer_kernel(tc, in_data, W_words, W_scales, bias, out):
         for q in range(4):
             nc.tensor.matmul(out=turned_banks[q][:, 2 * P : 4 * P], lhsT=zeros[:, 0:P], rhs=zeros[:, 0 : 2 * P], start=True, stop=True)
 
+        def buffer_matmul(q):
+            nc.tensor.matmul(out=turned_banks[q][:, 2 * P : 2 * P + BUFFER_N], lhsT=zeros[:, 0:P], rhs=zeros[:, 0:BUFFER_N], start=True, stop=True)
+
         def bias_to_partitions():
             nc.vector.tensor_copy(out=bias_rows_f32[:], in_=bias_rows[:])
             bias_cols = products.tile([P, BANK], F32, name="bias_cols", tag="bank")
@@ -124,7 +136,9 @@ def tile_middlelayer_kernel(tc, in_data, W_words, W_scales, bias, out):
             nc.vector.tensor_tensor(out=b2_minus_b1[:], in0=bias_cols[:, J_TILES : 2 * J_TILES], in1=neg_b1[:], op=ALU.add)
 
         def copy_on(engine, out_ap, in_ap):
-            if engine == "vector":
+            if engine == "gpsimd":
+                nc.gpsimd.tensor_scalar(out=out_ap, in0=in_ap, scalar1=1.0, scalar2=0.0, op0=ALU.mult, op1=ALU.add)
+            elif engine == "vector":
                 nc.vector.tensor_copy(out=out_ap, in_=in_ap)
             else:
                 nc.scalar.copy(out=out_ap, in_=in_ap)
@@ -227,6 +241,8 @@ def tile_middlelayer_kernel(tc, in_data, W_words, W_scales, bias, out):
                     bank = turned_banks[slot]
                     for a in range(2):
                         nc.tensor.transpose(out=bank[:, a * P : (a + 1) * P], in_=r_tiles[2 * h + a][:, q * P : (q + 1) * P], identity=identity[:])
+                    if slot == 3 and BUFFER_N:
+                        buffer_matmul(3)
                     copy_on(engines[slot % len(engines)],
                             rows[:, part * width + h * BANK : part * width + (h + 1) * BANK].rearrange("p (c e) -> p c e", e=2),
                             bank[:].rearrange("p (e c) -> p c e", e=2))
@@ -281,18 +297,18 @@ def tile_middlelayer_kernel(tc, in_data, W_words, W_scales, bias, out):
             nc.sync.dma_start(out=out_rows[bt * P : (bt + 1) * P, col : col + 2 * BANK], in_=rows[:])
 
         SPLIT = ("vector", "scalar")
-        imag = {0: take_imaginary(0, SPLIT)}
+        imag = {0: take_imaginary(0, HEAD_SPLIT)}
         grouped = {}
         for bt in range(HEAD_TILES):
             if bt + 1 < HEAD_TILES:
-                imag[bt + 1] = take_imaginary(bt + 1, SPLIT)
+                imag[bt + 1] = take_imaginary(bt + 1, HEAD_SPLIT)
             grouped[bt] = transpose_x(imag[bt], "scalar")
             if bt == 0:
                 bias_to_partitions()
             if bt >= 1:
                 quantise_x(bt - 1, grouped[bt - 1])
         quantise_x(HEAD_TILES - 1, grouped[HEAD_TILES - 1])
-        for c in range((J - UB) // BANK):
+        for c in HEAD_BIAS:
             for s in (1, 0):
                 spread_bias(s, c, "scalar")
 
@@ -317,8 +333,10 @@ def tile_middlelayer_kernel(tc, in_data, W_words, W_scales, bias, out):
         for i, (b_from, b_tiles, jt, n_j, part, parts) in enumerate(rounds):
             tile_x = X_AT.get(i)
             relu2 = fold_first(multiply_half(1, b_from, b_tiles, jt, n_j), b_tiles, jt)
-            if X_AT.get(i + 1) is not None:
-                imag[X_AT[i + 1]] = take_imaginary(X_AT[i + 1], SPLIT)
+            if X_AT.get(i + 1) is not None and IMAG_EARLY:
+                imag[X_AT[i + 1]] = take_imaginary(X_AT[i + 1], ROUND_SPLIT)
+            if pending and BUFFER_N:
+                buffer_matmul(0)
             if tile_x is not None:
                 grouped[tile_x] = transpose_x(imag[tile_x], "scalar")
             if pending:
@@ -329,8 +347,15 @@ def tile_middlelayer_kernel(tc, in_data, W_words, W_scales, bias, out):
             open_units.extend(fresh_units)
             fresh_units.clear()
             r = fold_second(multiply_half(0, b_from, b_tiles, jt, n_j), relu2, b_tiles, jt)
+            if X_AT.get(i + 1) is not None and not IMAG_EARLY:
+                imag[X_AT[i + 1]] = take_imaginary(X_AT[i + 1], ROUND_SPLIT)
+            if LATE_BIAS.get(i) is not None:
+                for s in (1, 0):
+                    spread_bias(s, LATE_BIAS[i], LATE_BIAS_ENGINES[s])
+            if tile_x is not None and QUANT_EARLY:
+                quantise_x(tile_x, grouped[tile_x])
             fresh_units.extend([(bt, c, unit_multiply(bt, c), kind) for bt, c, kind in UNITS_AT.get(i, ())])
-            if tile_x is not None:
+            if tile_x is not None and not QUANT_EARLY:
                 quantise_x(tile_x, grouped[tile_x])
             pending = (b_from, b_tiles, jt, n_j, r, part, parts)
         turn_and_store(*pending, SHARE)

from contextlib import ExitStack

import concourse.mybir as mybir
from concourse.masks import make_identity

F32 = mybir.dt.float32
BF16 = mybir.dt.bfloat16
I32 = mybir.dt.int32
U32 = mybir.dt.uint32
U8 = mybir.dt.uint8
FP8X4 = mybir.dt.float8_e4m3fn_x4
ALU = mybir.AluOpType
ACT = mybir.ActivationFunctionType

P = 128
B = 1024
K = 1024
N = 4096
J = N // 2
PASSES = K // (4 * P)
B_TILES = B // P
J_TILES = J // P
BANK = 512
JX = 1536
JX_TILES = JX // P
WIDE_ROWS = 3
PRODUCT_BANKS = 4

RUNS = ((0, 4), (4, 4))
HEAD_TILES = 4
X_AT = {2: 4, 3: 5, 4: 6, 5: 7}
UNITS_AT = {2: ((0, 0, "g"),), 3: ((1, 0, "g"),), 4: ((2, 0, "g"),), 5: ((3, 0, "g"),), 6: ((4, 0, "g"),), 7: ((5, 0, "g"),), 8: ((6, 0, "g"),), 9: ((7, 0, "g"),)}
BIAS_AT = -1
FOLD_BUFS = 4
FOLDED_BUFS = 8
ROWS_BUFS = 16
STORE_GROUPS = ((1, 1, 1, 1, 1, 1), (1, 1, 1, 1, 1, 1))
LOADS = (("x", 0), ("b",), ("x", 1), ("x", 2), ("x", 3), ("s",), ("w", 0, 2), ("w", 2, 4), ("x", 4), ("w", 4, 6), ("x", 5), ("w", 12, 16), ("w", 6, 8), ("x", 6), ("x", 7), ("w", 8, 12))
SHARE_FROM = 11
SHARE = ("scalar", "vector")
ROUNDS = ((0, 4, 0, 2), (0, 4, 2, 2), (0, 4, 4, 2), (0, 4, 6, 2), (0, 4, 8, 2), (0, 4, 10, 2), (4, 4, 0, 2), (4, 4, 2, 2), (4, 4, 4, 2), (4, 4, 6, 2), (4, 4, 8, 2), (4, 4, 10, 2))
UB = 1536
SUMS_BUFS = 5
WIDE_BUFS = 4
HEAD_BIAS = (0,)
LATE_BIAS = {}
LATE_BIAS_ENGINES = ("vector", "scalar")
BUFFER_N = 32
HEAD_SPLIT = ("vector", "scalar")
ROUND_SPLIT = ("vector", "scalar")
IMAG_EARLY = True
QUANT_EARLY = True

FLOPS = 2 * B * K * N


def tile_middlelayer_kernel(tc, in_data, W_words, W_scales, bias, out):
    nc = tc.nc
    out_rows = out.rearrange("b n o -> b (n o)")

    with ExitStack() as ctx:
        ctx.enter_context(tc.manual_schedule())
        keep = ctx.enter_context(tc.tile_pool(name="keep", bufs=1))
        x_stage = ctx.enter_context(tc.tile_pool(name="x_stage", bufs=3))
        fold = ctx.enter_context(tc.tile_pool(name="fold", bufs=FOLD_BUFS))
        folded = ctx.enter_context(tc.tile_pool(name="folded", bufs=FOLDED_BUFS))
        rows_out = ctx.enter_context(tc.tile_pool(name="rows_out", bufs=ROWS_BUFS))
        sums_pool = ctx.enter_context(tc.tile_pool(name="sums_pool", bufs=SUMS_BUFS))
        wide_pool = ctx.enter_context(tc.tile_pool(name="wide_pool", bufs=WIDE_BUFS))
        products = ctx.enter_context(tc.psum_pool(name="products", bufs=PRODUCT_BANKS))
        turned = ctx.enter_context(tc.psum_pool(name="turned", bufs=1))

        x_raw = [keep.tile([P, 2 * K], BF16, name="x_raw%d" % bt) for bt in range(B_TILES)]
        x_codes = keep.tile([P, PASSES, B], U32, name="x_codes", align_bytes=64)
        x_scales = keep.tile([P, PASSES, B], U8, name="x_scales", align_bytes=64)
        w_codes = keep.tile([P, PASSES, N], U32, name="w_codes", align_bytes=64)
        w_scales = keep.tile([P, N], U8, name="w_scales", align_bytes=64)
        identity = keep.tile([P, P], F32, name="identity")
        zeros = keep.tile([P, 2 * BANK], BF16, name="zeros")
        bias_rows = keep.tile([P, P], BF16, name="bias_rows")
        bias_rows_f32 = keep.tile([P, P], F32, name="bias_rows_f32")
        neg_b1 = keep.tile([P, J_TILES], F32, name="neg_b1")
        b2_minus_b1 = keep.tile([P, J_TILES], F32, name="b2_minus_b1")
        identity_bf16 = keep.tile([P, P], BF16, name="identity_bf16")
        bias_all = keep.tile([P, 2, J - UB], F32, name="bias_all")
        wide_rows = [keep.tile([P, 2, BANK], F32, name="wide_rows%d" % i) for i in range(WIDE_ROWS)]

        def load_x(bt):
            nc.sync.dma_start(out=x_raw[bt][:], in_=in_data[bt * P : (bt + 1) * P, :])

        def load_w(j_from, j_to):
            cols = slice(j_from * P, j_to * P)
            for g in range(PASSES):
                words = W_words[g].rearrange("p n t -> p (n t)").bitcast(I32)
                nc.sync.dma_start(
                    out=w_codes[:, g, :].bitcast(I32).rearrange("p (s n) -> p s n", s=2)[:, :, cols],
                    in_=words.rearrange("p (s n) -> p s n", s=2)[:, :, cols],
                )

        def load_scales():
            for quadrant in range(4):
                nc.sync.dma_start(
                    out=w_scales[32 * quadrant : 32 * quadrant + 4 * PASSES, :].bitcast(I32),
                    in_=W_scales[:, 4 * quadrant : 4 * quadrant + 4, :].bitcast(I32),
                )

        nc.vector.memset(bias_rows[:], 0.0)
        for what in LOADS:
            if what[0] == "x":
                load_x(what[1])
            elif what[0] == "w":
                load_w(what[1], what[2])
            elif what[0] == "b":
                nc.sync.dma_start(out=bias_rows[0 : N // P, :], in_=bias.rearrange("(r c) -> r c", c=P))
            else:
                make_identity(nc, identity[:])
                make_identity(nc, identity_bf16[:])
                nc.vector.memset(zeros[:].bitcast(I32), 0)
                nc.vector.memset(w_scales[:].bitcast(I32), 0)
                for rows in wide_rows:
                    nc.scalar.copy(out=rows[:, 1, :], in_=zeros[:, 0:BANK])
                load_scales()

        turned_banks = [turned.tile([P, BANK], F32, name="turned%d" % q) for q in range(4)]
        for q in range(4):
            nc.tensor.matmul(out=turned_banks[q][:, 2 * P : 4 * P], lhsT=zeros[:, 0:P], rhs=zeros[:, 0 : 2 * P], start=True, stop=True)

        def buffer_matmul(q):
            nc.tensor.matmul(out=turned_banks[q][:, 2 * P : 2 * P + BUFFER_N], lhsT=zeros[:, 0:P], rhs=zeros[:, 0:BUFFER_N], start=True, stop=True)

        def bias_to_partitions():
            nc.vector.tensor_copy(out=bias_rows_f32[:], in_=bias_rows[:])
            bias_cols = products.tile([P, BANK], F32, name="bias_cols", tag="bank")
            nc.tensor.transpose(out=bias_cols[:, 0:P], in_=bias_rows_f32[:], identity=identity[:])
            nc.vector.tensor_scalar(out=neg_b1[:], in0=bias_cols[:, 0:J_TILES], scalar1=-1.0, scalar2=None, op0=ALU.mult)
            nc.vector.tensor_tensor(out=b2_minus_b1[:], in0=bias_cols[:, J_TILES : 2 * J_TILES], in1=neg_b1[:], op=ALU.add)

        def copy_on(engine, out_ap, in_ap):
            if engine == "gpsimd":
                nc.gpsimd.tensor_scalar(out=out_ap, in0=in_ap, scalar1=1.0, scalar2=0.0, op0=ALU.mult, op1=ALU.add)
            elif engine == "vector":
                nc.vector.tensor_copy(out=out_ap, in_=in_ap)
            else:
                nc.scalar.copy(out=out_ap, in_=in_ap)

        def spread_bias(s, c, engine):
            bank = products.tile([P, BANK], F32, name="bias_bank", tag="bank")
            cols = slice(c * BANK, (c + 1) * BANK)
            for i in range(BANK // P):
                row = (s * J + UB + c * BANK) // P + i
                nc.tensor.matmul(
                    out=bank[:, i * P : (i + 1) * P],
                    lhsT=identity_bf16[:, row : row + 1].to_broadcast([P, P]),
                    rhs=bias_rows[:],
                    start=True,
                    stop=True,
                )
            copy_on(engine, bias_all[:, s, cols], bank[:])

        def take_imaginary(bt, engines):
            x_imag = x_stage.tile([P, PASSES, 2, P, 2], BF16, name="x_imag")
            pairs = x_raw[bt][:].rearrange("b (g p u e c) -> b g u p e c", g=PASSES, p=P, u=2, e=2, c=2)
            for g in range(PASSES):
                copy_on(engines[g], x_imag[:, g], pairs[:, g, :, :, :, 1])
            return x_imag

        def transpose_x(x_imag, engine):
            words = x_imag[:].rearrange("b g u p e -> b (g u p e)").bitcast(F32)
            x_turned = products.tile([P, BANK], F32, name="x_turned", tag="bank")
            for gu in range(2 * PASSES):
                cols = slice(gu * P, (gu + 1) * P)
                nc.tensor.transpose(out=x_turned[:, cols], in_=words[:, cols], identity=identity[:])
            grouped = x_stage.tile([P, PASSES, P, 4], BF16, name="grouped", align_bytes=64)
            copy_on(
                engine,
                grouped[:].rearrange("p g b t -> p g (b t)").bitcast(F32).rearrange("p g (b u) -> p g b u", u=2),
                x_turned[:].rearrange("p (g u b) -> p g b u", g=PASSES, u=2),
            )
            return grouped

        def quantise_x(bt, grouped):
            rows = slice(bt * P, (bt + 1) * P)
            for g in range(PASSES):
                nc.vector.quantize_mx(
                    out=x_codes[:, g, rows].bitcast(FP8X4),
                    scales=x_scales[:, g, rows],
                    in_=grouped[:, g].rearrange("p b t -> p (b t)"),
                )

        def product(acc, n_tile, b_from, b_tiles):
            n_cols = slice(n_tile * P, (n_tile + 1) * P)
            b_cols = slice(b_from * P, (b_from + b_tiles) * P)
            for g in range(PASSES):
                nc.tensor.matmul_mx(
                    out=acc,
                    lhsT=w_codes[:, g, n_cols].bitcast(FP8X4),
                    lhsT_scale=w_scales[4 * g : P, n_cols],
                    rhs=x_codes[:, g, b_cols].bitcast(FP8X4),
                    rhs_scale=x_scales[:, g, b_cols],
                    start=(g == 0),
                    stop=(g == PASSES - 1),
                )

        def multiply_half(half, b_from, b_tiles, jt, n_j):
            width = b_tiles * P
            accs = []
            for a in range(n_j):
                bank = products.tile([P, BANK], F32, name="product", tag="bank")
                accs.append(bank[:, 0:width])
                product(accs[a], half * J_TILES + jt + a, b_from, b_tiles)
            return accs

        def fold_first(accs, b_tiles, jt):
            relu2 = []
            for a, acc in enumerate(accs):
                t = fold.tile([P, b_tiles * P], F32, name="relu2")
                nc.vector.tensor_scalar(out=t[:], in0=acc, scalar1=b2_minus_b1[:, jt + a : jt + a + 1],
                                        scalar2=neg_b1[:, jt + a : jt + a + 1], op0=ALU.add, op1=ALU.max)
                relu2.append(t)
            return relu2

        def fold_second(accs, relu2, b_tiles, jt):
            r_tiles = []
            for a, acc in enumerate(accs):
                t = folded.tile([P, b_tiles * P], F32, name="r_tile")
                nc.vector.scalar_tensor_tensor(out=t[:], in0=acc, scalar=neg_b1[:, jt + a : jt + a + 1],
                                               in1=relu2[a][:], op0=ALU.max, op1=ALU.subtract)
                r_tiles.append(t)
            return r_tiles

        shared_rows = {}

        def turn_and_store(b_from, b_tiles, jt, n_j, r_tiles, part, parts, engines):
            slot = 0
            width = 2 * P * n_j
            for q in range(b_tiles):
                if part == 0:
                    shared_rows[q] = rows_out.tile([P, width * parts], F32, name="rows")
                rows = shared_rows[q]
                for h in range(n_j // 2):
                    bank = turned_banks[slot]
                    for a in range(2):
                        nc.tensor.transpose(out=bank[:, a * P : (a + 1) * P], in_=r_tiles[2 * h + a][:, q * P : (q + 1) * P], identity=identity[:])
                    if slot == 3 and BUFFER_N:
                        buffer_matmul(3)
                    copy_on(engines[slot % len(engines)],
                            rows[:, part * width + h * BANK : part * width + (h + 1) * BANK].rearrange("p (c e) -> p c e", e=2),
                            bank[:].rearrange("p (e c) -> p c e", e=2))
                    slot += 1
                bt = b_from + q
                if part == parts - 1:
                    col = 2 * (jt + n_j) * P
                    nc.sync.dma_start(out=out_rows[bt * P : (bt + 1) * P, col - width * parts : col], in_=rows[:])

        def unit_multiply(bt, c):
            b_cols = slice(bt * P, (bt + 1) * P)
            sums = sums_pool.tile([P, 2, BANK], F32, name="sums")
            banks = {}
            for s in (1, 0):
                banks[s] = products.tile([P, BANK], F32, name="unit_bank", tag="bank")
                n_cols = slice(s * J + UB + c * BANK, s * J + UB + (c + 1) * BANK)
                for g in range(PASSES):
                    nc.tensor.matmul_mx(
                        out=banks[s][:],
                        lhsT=x_codes[:, g, b_cols].bitcast(FP8X4),
                        lhsT_scale=x_scales[:, g, b_cols],
                        rhs=w_codes[:, g, n_cols].bitcast(FP8X4),
                        rhs_scale=w_scales[4 * g : P, n_cols],
                        start=(g == 0),
                        stop=(g == PASSES - 1),
                    )
            for s in (1, 0):
                nc.vector.tensor_tensor(out=sums[:, s, :], in0=banks[s][:], in1=bias_all[:, s, c * BANK : (c + 1) * BANK], op=ALU.add)
            return sums

        def unit_relu(sums, kind):
            if kind == "g":
                nc.scalar.activation(out=sums[:], in_=sums[:], func=ACT.Relu)
            else:
                nc.scalar.activation(out=sums[:, 1, :], in_=sums[:, 1, :], func=ACT.Relu)

        used = []

        def unit_finish(bt, c, sums, kind):
            pair = wide_rows[len(used) % WIDE_ROWS]
            used.append(0)
            if kind == "g":
                nc.gpsimd.tensor_tensor(out=pair[:, 0, :], in0=sums[:, 0, :], in1=sums[:, 1, :], op=ALU.subtract)
            else:
                nc.vector.scalar_tensor_tensor(out=pair[:, 0, :], in0=sums[:, 0, :], scalar=0.0, in1=sums[:, 1, :], op0=ALU.max, op1=ALU.subtract)
            rows = wide_pool.tile([P, 2 * BANK], F32, name="wide")
            if kind == "v":
                nc.scalar.copy(out=rows[:].rearrange("p (c e) -> p c e", e=2), in_=pair[:].rearrange("p e c -> p c e"))
            else:
                nc.gpsimd.tensor_scalar(out=rows[:].rearrange("p (c e) -> p c e", e=2), in0=pair[:].rearrange("p e c -> p c e"), scalar1=1.0, scalar2=0.0, op0=ALU.mult, op1=ALU.add)
            col = 2 * (UB + c * BANK)
            nc.sync.dma_start(out=out_rows[bt * P : (bt + 1) * P, col : col + 2 * BANK], in_=rows[:])

        SPLIT = ("vector", "scalar")
        imag = {0: take_imaginary(0, HEAD_SPLIT)}
        grouped = {}
        for bt in range(HEAD_TILES):
            if bt + 1 < HEAD_TILES:
                imag[bt + 1] = take_imaginary(bt + 1, HEAD_SPLIT)
            grouped[bt] = transpose_x(imag[bt], "scalar")
            if bt == 0:
                bias_to_partitions()
            if bt >= 1:
                quantise_x(bt - 1, grouped[bt - 1])
        quantise_x(HEAD_TILES - 1, grouped[HEAD_TILES - 1])
        for c in HEAD_BIAS:
            for s in (1, 0):
                spread_bias(s, c, "scalar")

        rounds = [rd + (0, 1) for rd in ROUNDS]
        pending = None
        open_units = []

        def nothing():
            return None

        def finish_early():
            for u in [u for u in open_units if u[3] != "g"]:
                unit_finish(*u)
                open_units.remove(u)

        def finish_units():
            for u in open_units:
                unit_finish(*u)
            open_units.clear()

        fresh_units = []
        for i, (b_from, b_tiles, jt, n_j, part, parts) in enumerate(rounds):
            tile_x = X_AT.get(i)
            relu2 = fold_first(multiply_half(1, b_from, b_tiles, jt, n_j), b_tiles, jt)
            if X_AT.get(i + 1) is not None and IMAG_EARLY:
                imag[X_AT[i + 1]] = take_imaginary(X_AT[i + 1], ROUND_SPLIT)
            if pending and BUFFER_N:
                buffer_matmul(0)
            if tile_x is not None:
                grouped[tile_x] = transpose_x(imag[tile_x], "scalar")
            if pending:
                turn_and_store(*pending, ("scalar",) if i < SHARE_FROM else SHARE)
            finish_units()
            for u in fresh_units:
                unit_relu(u[2], u[3])
            open_units.extend(fresh_units)
            fresh_units.clear()
            r = fold_second(multiply_half(0, b_from, b_tiles, jt, n_j), relu2, b_tiles, jt)
            if X_AT.get(i + 1) is not None and not IMAG_EARLY:
                imag[X_AT[i + 1]] = take_imaginary(X_AT[i + 1], ROUND_SPLIT)
            if LATE_BIAS.get(i) is not None:
                for s in (1, 0):
                    spread_bias(s, LATE_BIAS[i], LATE_BIAS_ENGINES[s])
            if tile_x is not None and QUANT_EARLY:
                quantise_x(tile_x, grouped[tile_x])
            fresh_units.extend([(bt, c, unit_multiply(bt, c), kind) for bt, c, kind in UNITS_AT.get(i, ())])
            if tile_x is not None and not QUANT_EARLY:
                quantise_x(tile_x, grouped[tile_x])
            pending = (b_from, b_tiles, jt, n_j, r, part, parts)
        turn_and_store(*pending, SHARE)
        finish_units()
        for u in fresh_units:
            unit_relu(u[2], u[3])
            unit_finish(*u)
